import numpy as np
import ml_dtypes


def mxq(x, axis, fmt="e4m3"):
    dtype, down = {"e4m3": (ml_dtypes.float8_e4m3fn, 7), "e5m2": (ml_dtypes.float8_e5m2, 14)}[fmt]
    v = np.moveaxis(np.asarray(x, np.float32).astype(ml_dtypes.bfloat16).astype(np.float64), axis, -1)
    blocks = v.reshape(v.shape[:-1] + (-1, 32))
    amax = np.abs(blocks).max(-1, keepdims=True)
    byte = np.maximum(np.where(amax > 0, np.frexp(amax)[1] - 1 + 127, 0) - down, 1)
    scale = np.exp2(byte - 127.0)
    codes = (blocks / scale).astype(np.float32).astype(dtype).astype(np.float64)
    return np.moveaxis((codes * scale).reshape(v.shape), -1, axis)


WIDE = False


def mx_kscale(k):
    if not WIDE:
        return np.ones(k)
    levels = np.array([10, -10, 5, -5, 0])
    a = np.random.permutation(np.resize(levels, k // 512 * 4)).reshape(k // 512, 4)
    idx = np.arange(k)
    return np.exp2(a[idx // 512, idx % 128 // 32])


BF16 = ml_dtypes.bfloat16


def bf(x):
    return np.asarray(x, np.float32).astype(BF16)


def f64(x):
    return np.asarray(x).astype(np.float64)


B, L, D, F = 128, 1, 8192, 512
EPS = 1e-12


def l2norm(w, axis):
    n = np.sqrt(np.sum(w * w, axis=axis, keepdims=True))
    return w / np.maximum(n, EPS)


def silu(z):
    return z / (1.0 + np.exp(-z))


def draw_w(k, n, s):
    a = np.random.standard_normal((L, k, n)) / s[:, None]
    return a / np.sqrt(np.sum(a * a, axis=1, keepdims=True)) * np.exp2(np.random.randint(-1, 2, (L, 1, n)))


def draw_gain():
    return np.random.choice([-1.0, 1.0], (1, F)) * (1.0 + 0.1 * np.random.standard_normal((1, F)))


def setup_inputs():
    s, t = mx_kscale(D), mx_kscale(F)
    c = np.sqrt(np.mean(1.0 / s**2))
    return {'x': bf(np.random.standard_normal((B, L, D)) * s),
            'W_gate': bf(draw_w(D, F, s)),
            'W_up': bf(draw_w(D, F, s)),
            'W_down': bf(draw_w(F, D, t)),
            's_u': bf(draw_gain() * c * t),
            's_v': bf(draw_gain() * c * 1.5 / np.sqrt(D))}


def reference(x, W_gate, W_up, W_down, s_u, s_v):
    Wg = l2norm(f64(W_gate), 1)
    Wu = l2norm(f64(W_up), 1)
    Wd = l2norm(f64(W_down), 1)
    xq = mxq(f64(x), 2, 'e4m3').transpose(1, 0, 2)
    u = xq @ mxq(Wg, 1, 'e4m3')
    v = xq @ mxq(Wu, 1, 'e4m3')
    u_scale = np.abs(f64(s_u)) * 1.0
    v_scale = np.abs(f64(s_v)) * np.sqrt(D)
    h = silu(v_scale * v) * (u_scale * u)
    out = (mxq(h, 2, 'e4m3') @ mxq(Wd, 1, 'e4m3')).transpose(1, 0, 2)
    return l2norm(out, -1)

@@ -1,0 +1,367 @@
+import math
+from contextlib import ExitStack
+
+import concourse.mybir as mybir
+from concourse.masks import make_identity
+
+F32 = mybir.dt.float32
+BF16 = mybir.dt.bfloat16
+U32 = mybir.dt.uint32
+U8 = mybir.dt.uint8
+FP8X4 = mybir.dt.float8_e4m3fn_x4
+ACT = mybir.ActivationFunctionType
+ALU = mybir.AluOpType
+AX = mybir.AxisListType
+
+P = 128
+PACK = 4
+K_PASS = P * PACK
+TOKENS = 128
+D_MODEL = 8192
+HIDDEN = 512
+PASSES = D_MODEL // K_PASS
+CHUNK = 4
+PAIRS = 2 * P
+BANK = 512
+D_LOAD = 2048
+NORM_FLOOR = 1e-12
+GPSIMD_EVERY = 3
+
+FLOPS = 3 * 2 * TOKENS * D_MODEL * HIDDEN
+
+
+def tile_npertokenswishglu_k_kernel(tc, x, W_gate, W_up, W_down, s_u, s_v, out):
+    nc = tc.nc
+    with ExitStack() as ctx:
+        const = ctx.enter_context(tc.tile_pool(name="const", bufs=1))
+        big = ctx.enter_context(tc.tile_pool(name="big", bufs=8))
+        factor_pool = ctx.enter_context(tc.tile_pool(name="factor_pool", bufs=3))
+        work = ctx.enter_context(tc.tile_pool(name="work", bufs=3))
+        junk = ctx.enter_context(tc.tile_pool(name="junk", bufs=4))
+        small = ctx.enter_context(tc.tile_pool(name="small", bufs=4))
+        turned_pool = ctx.enter_context(tc.psum_pool(name="turned_pool", bufs=3))
+        spread_pool = ctx.enter_context(tc.psum_pool(name="spread_pool", bufs=3))
+        acc_pool = ctx.enter_context(tc.psum_pool(name="acc_pool", bufs=2))
+
+        ident = const.tile([P, P], F32, tag="ident")
+        make_identity(nc, ident[:])
+        ident_bf = const.tile([P, P], BF16, tag="ident_bf")
+        make_identity(nc, ident_bf[:])
+        minus_half = const.tile([P, 4], F32, tag="minus_half")
+        nc.vector.memset(minus_half[:], -0.5)
+
+        def add_up_squares(bank, sums):
+            halves = bank[:].bitcast(BF16).rearrange("q (k e) -> q k e", e=2)
+            for e in range(2):
+                squares = junk.tile([P, BANK], BF16, tag="squares")
+                nc.scalar.activation(
+                    out=squares[:], in_=halves[:, :, e], func=ACT.Square, accum_out=sums[e]
+                )
+
+        def one_over_norm(sum_of_squares, width):
+            floored = small.tile([P, width], F32, tag="floored")
+            nc.gpsimd.tensor_scalar_max(
+                out=floored[:], in0=sum_of_squares, scalar1=NORM_FLOOR * NORM_FLOOR
+            )
+            inverse = small.tile([P, width], F32, tag="inverse")
+            nc.gpsimd.tensor_tensor(
+                out=inverse[:], in0=floored[:], in1=minus_half[:, 0:width], op=ALU.pow
+            )
+            return inverse
+
+        def spread_over_partitions(inverse, width):
+            spread = spread_pool.tile([P, width, P], F32, tag="spread")
+            for c in range(width):
+                nc.tensor.transpose(
+                    spread[:, c, :], inverse[:, c : c + 1].to_broadcast([P, P]), ident[:]
+                )
+            return spread
+
+        def for_gpsimd(group):
+            return group % GPSIMD_EVERY == GPSIMD_EVERY - 1
+
+        def copy_for_gpsimd(spread_pair):
+            factors = factor_pool.tile([P, 2, P], F32, tag="factors")
+            nc.vector.tensor_copy(out=factors[:], in_=spread_pair)
+            return factors
+
+        def scale_and_group(engine, grouped_cols, raw_rows, spread_pair):
+            engine.tensor_tensor(
+                out=grouped_cols.rearrange("p (q e j) -> p q e j", e=2, j=PACK),
+                in0=raw_rows.rearrange("p j (q e) -> p q e j", e=2),
+                in1=spread_pair.rearrange("p e q -> p q e")
+                .unsqueeze(3)
+                .to_broadcast([P, P, 2, PACK]),
+                op=ALU.mult,
+            )
+
+        gain_rows = const.tile([P, P], BF16, tag="gain_rows")
+        nc.vector.memset(gain_rows[:], 0.0)
+        nc.scalar.dma_start(out=gain_rows[0:4, :], in_=s_u.rearrange("o (t c) -> (o t) c", c=P))
+        nc.scalar.dma_start(out=gain_rows[4:8, :], in_=s_v.rearrange("o (t c) -> (o t) c", c=P))
+
+        gate_view = W_gate.rearrange("l (g p j) f -> p (l g) (j f)", p=P, j=PACK)
+        up_view = W_up.rearrange("l (g p j) f -> p (l g) (j f)", p=P, j=PACK)
+
+        def load_gate_or_up(view, c):
+            raw = big.tile([P, CHUNK, PACK, HIDDEN], BF16, tag="big")
+            for i in range(CHUNK):
+                nc.sync.dma_start(
+                    out=raw[:, i, :, :].rearrange("p j f -> p (j f)"), in_=view[:, c * CHUNK + i, :]
+                )
+            return raw
+
+        gate_raw = [load_gate_or_up(gate_view, c) for c in range(PASSES // CHUNK)]
+        x_raw = const.tile([P, D_MODEL], BF16, tag="x_raw")
+        nc.sync.dma_start(out=x_raw[:], in_=x.rearrange("b l d -> b (l d)"))
+        up_raw = [load_gate_or_up(up_view, c) for c in range(PASSES // CHUNK)]
+        x_words = x_raw[:].bitcast(F32).rearrange("b (g p u) -> b g u p", p=P, u=2)
+        x_codes = const.tile([P, PASSES, TOKENS], U32, tag="x_codes", align_bytes=64)
+        x_plane = const.tile([P, PASSES, TOKENS], U8, tag="x_plane", align_bytes=64)
+
+        def quantise_x(c):
+            x_grouped = work.tile([P, CHUNK, TOKENS * PACK], BF16, tag="grouped", align_bytes=64)
+            x_grouped_words = x_grouped[:].bitcast(F32)
+            for h in range(2):
+                bank = turned_pool.tile([P, BANK], F32, tag="turned")
+                for i in range(2):
+                    for u in range(2):
+                        col = (2 * i + u) * P
+                        nc.tensor.transpose(
+                            bank[:, col : col + P], x_words[:, c * CHUNK + 2 * h + i, u, :], ident[:]
+                        )
+                nc.vector.tensor_copy(
+                    out=x_grouped_words[:, 2 * h : 2 * h + 2, :].rearrange(
+                        "p i (b u) -> p i b u", u=2
+                    ),
+                    in_=bank[:].rearrange("p (i u b) -> p i b u", i=2, u=2),
+                )
+            nc.vector.quantize_mx(
+                out=x_codes[:, c * CHUNK : (c + 1) * CHUNK, :]
+                .rearrange("p g b -> p (g b)")
+                .bitcast(FP8X4),
+                scales=x_plane[:, c * CHUNK : (c + 1) * CHUNK, :].rearrange("p g b -> p (g b)"),
+                in_=x_grouped[:].rearrange("p g n -> p (g n)"),
+            )
+
+        def prepare_gains():
+            gain_cols = turned_pool.tile([P, P], BF16, tag="turned")
+            nc.tensor.transpose(gain_cols[:], gain_rows[:], ident_bf[:])
+            gains = const.tile([P, 8], F32, tag="gains")
+            nc.vector.tensor_copy(out=gains[:], in_=gain_cols[:, 0:8])
+            nc.vector.scalar_tensor_tensor(
+                out=sizes[:], in0=gains[:], scalar=-1.0, in1=gains[:], op0=ALU.mult, op1=ALU.max
+            )
+            nc.vector.tensor_scalar_mul(
+                out=sizes[:, 4:8], in0=sizes[:, 4:8], scalar1=math.sqrt(float(D_MODEL))
+            )
+
+        sizes = const.tile([P, 8], F32, tag="sizes")
+
+        def gate_up_norms(raw, half):
+            sums = small.tile([P, 2, PASSES], F32, tag="sums")
+            for g in range(PASSES):
+                words = raw[g // CHUNK][:, g % CHUNK, :, :].bitcast(F32)
+                bank = turned_pool.tile([P, BANK], F32, tag="turned")
+                for j in range(PACK):
+                    nc.tensor.transpose(
+                        bank[:, j * P : (j + 1) * P], words[:, j, half * P : (half + 1) * P], ident[:]
+                    )
+                add_up_squares(bank, [sums[:, e, g : g + 1] for e in range(2)])
+            total = small.tile([P, 2], F32, tag="total")
+            nc.vector.tensor_reduce(out=total[:], in_=sums[:], axis=AX.X, op=ALU.add)
+            return spread_over_partitions(one_over_norm(total[:], 2), 2)
+
+        def gate_up_products(raw, half, spread):
+            acc = [acc_pool.tile([P, TOKENS], F32, tag="acc", name="acc%d" % m) for m in range(2)]
+            grouped = [None] * (PASSES // CHUNK)
+            factors = copy_for_gpsimd(spread[:])
+
+            def scale(c):
+                grouped[c] = work.tile(
+                    [P, CHUNK, PAIRS * PACK], BF16, tag="grouped", align_bytes=64, name="grouped"
+                )
+                for i in range(CHUNK):
+                    on_gpsimd = for_gpsimd(c * CHUNK + i)
+                    scale_and_group(
+                        nc.gpsimd if on_gpsimd else nc.vector,
+                        grouped[c][:, i, :],
+                        raw[c][:, i, :, half * PAIRS : (half + 1) * PAIRS],
+                        factors[:] if on_gpsimd else spread[:],
+                    )
+
+            def quantise_and_multiply(c):
+                codes = work.tile([P, CHUNK, PAIRS], U32, tag="codes", align_bytes=64)
+                plane = work.tile([P, CHUNK, PAIRS], U8, tag="plane", align_bytes=64)
+                nc.vector.quantize_mx(
+                    out=codes[:].rearrange("p g w -> p (g w)").bitcast(FP8X4),
+                    scales=plane[:].rearrange("p g w -> p (g w)"),
+                    in_=grouped[c][:].rearrange("p g n -> p (g n)"),
+                )
+                for m in range(2):
+                    for i in range(CHUNK):
+                        g = c * CHUNK + i
+                        nc.tensor.matmul_mx(
+                            out=acc[m][:],
+                            lhsT=codes[:, i, m * P : (m + 1) * P].bitcast(FP8X4),
+                            lhsT_scale=plane[:, i, m * P : (m + 1) * P],
+                            rhs=x_codes[:, g, :].bitcast(FP8X4),
+                            rhs_scale=x_plane[:, g, :],
+                            start=(g == 0),
+                            stop=(g == PASSES - 1),
+                        )
+
+            scale(0)
+            for c in range(1, PASSES // CHUNK):
+                scale(c)
+                quantise_and_multiply(c - 1)
+            quantise_and_multiply(PASSES // CHUNK - 1)
+            return acc
+
+        u_scaled = const.tile([P, PACK, TOKENS], F32, tag="u_scaled")
+        h_grouped = const.tile([P, TOKENS, PACK], BF16, tag="h_grouped", align_bytes=64)
+
+        def keep_gate(half, acc):
+            for m in range(2):
+                t = 2 * half + m
+                nc.scalar.activation(
+                    out=u_scaled[:, t, :], in_=acc[m][:], func=ACT.Copy, scale=sizes[:, t : t + 1]
+                )
+
+        def make_hidden(half, acc):
+            for m in range(2):
+                t = 2 * half + m
+                swish = small.tile([P, TOKENS], F32, tag="swish")
+                nc.scalar.activation(
+                    out=swish[:], in_=acc[m][:], func=ACT.Silu, scale=sizes[:, 4 + t : 5 + t]
+                )
+                nc.vector.tensor_tensor(
+                    out=h_grouped[:, :, t], in0=swish[:], in1=u_scaled[:, t, :], op=ALU.mult
+                )
+
+        gate_spread_0 = gate_up_norms(gate_raw, 0)
+        for c in range(PASSES // CHUNK):
+            quantise_x(c)
+        prepare_gains()
+        gate_spread_1 = gate_up_norms(gate_raw, 1)
+        keep_gate(0, gate_up_products(gate_raw, 0, gate_spread_0))
+        up_spread_0 = gate_up_norms(up_raw, 0)
+        keep_gate(1, gate_up_products(gate_raw, 1, gate_spread_1))
+
+        down_view = W_down.rearrange("l (t p) d -> p (l t) d", p=P)
+        down_raw = []
+        for c in range(D_MODEL // D_LOAD):
+            raw = big.tile([P, PACK, D_LOAD], BF16, tag="big", name="down_raw")
+            nc.sync.dma_start(out=raw[:], in_=down_view[:, :, c * D_LOAD : (c + 1) * D_LOAD])
+            down_raw.append(raw)
+
+        BLOCKS = D_MODEL // BANK
+        PER_LOAD = D_LOAD // BANK
+        down_sums = [None] * BLOCKS
+        down_spread = [None] * BLOCKS
+        down_grouped = [None] * BLOCKS
+        down_factors_sb = [None] * (2 * BLOCKS)
+
+        def down_rows(b, unit):
+            first = (b % PER_LOAD) * BANK + unit * PAIRS
+            return down_raw[b // PER_LOAD][:, :, first : first + PAIRS]
+
+        def down_squares(b):
+            down_sums[b] = small.tile([P, 4], F32, tag="down_sums", name="down_sums")
+            for unit in range(2):
+                words = down_rows(b, unit).bitcast(F32)
+                bank = turned_pool.tile([P, BANK], F32, tag="turned")
+                for t in range(PACK):
+                    nc.tensor.transpose(bank[:, t * P : (t + 1) * P], words[:, t, :], ident[:])
+                add_up_squares(
+                    bank, [down_sums[b][:, 2 * unit + e : 2 * unit + e + 1] for e in range(2)]
+                )
+
+        def down_factors(b):
+            down_spread[b] = spread_over_partitions(one_over_norm(down_sums[b][:], 4), 4)
+            for unit in range(2):
+                if for_gpsimd(2 * b + unit):
+                    down_factors_sb[2 * b + unit] = copy_for_gpsimd(
+                        down_spread[b][:, 2 * unit : 2 * unit + 2, :]
+                    )
+
+        def down_scale(b):
+            down_grouped[b] = work.tile(
+                [P, 2, PAIRS * PACK], BF16, tag="grouped", align_bytes=64, name="down_grouped"
+            )
+            for unit in range(2):
+                on_gpsimd = for_gpsimd(2 * b + unit)
+                scale_and_group(
+                    nc.gpsimd if on_gpsimd else nc.vector,
+                    down_grouped[b][:, unit, :],
+                    down_rows(b, unit),
+                    down_factors_sb[2 * b + unit][:]
+                    if on_gpsimd
+                    else down_spread[b][:, 2 * unit : 2 * unit + 2, :],
+                )
+
+        up_spread_1 = gate_up_norms(up_raw, 1)
+        make_hidden(0, gate_up_products(up_raw, 0, up_spread_0))
+        down_squares(0)
+        down_squares(1)
+        down_factors(0)
+        make_hidden(1, gate_up_products(up_raw, 1, up_spread_1))
+
+        h_codes = const.tile([P, TOKENS], U32, tag="h_codes", align_bytes=64)
+        h_plane = const.tile([P, TOKENS], U8, tag="h_plane", align_bytes=64)
+        nc.vector.quantize_mx(
+            out=h_codes[:].bitcast(FP8X4),
+            scales=h_plane[:],
+            in_=h_grouped[:].rearrange("p b t -> p (b t)"),
+        )
+
+        O_HALF = D_MODEL // 2
+        o_sb = [big.tile([P, O_HALF], F32, tag="big", name="o_sb%d" % i) for i in range(2)]
+        o_squares = const.tile([P, BLOCKS], F32, tag="o_squares")
+
+        def o_cols(first, width):
+            return o_sb[first // O_HALF][:, first % O_HALF : first % O_HALF + width]
+
+        def down_product(b):
+            codes = work.tile([P, BANK], U32, tag="codes", align_bytes=64)
+            plane = work.tile([P, BANK], U8, tag="plane", align_bytes=64)
+            nc.vector.quantize_mx(
+                out=codes[:].bitcast(FP8X4),
+                scales=plane[:],
+                in_=down_grouped[b][:].rearrange("p u n -> p (u n)"),
+            )
+            o_bank = acc_pool.tile([P, BANK], F32, tag="acc")
+            nc.tensor.matmul_mx(
+                out=o_bank[:],
+                lhsT=h_codes[:].bitcast(FP8X4),
+                lhsT_scale=h_plane[:],
+                rhs=codes[:].bitcast(FP8X4),
+                rhs_scale=plane[:],
+                start=True,
+                stop=True,
+            )
+            nc.scalar.copy(out=o_cols(b * BANK, BANK), in_=o_bank[:])
+            squares = junk.tile([P, BANK], BF16, tag="squares")
+            nc.scalar.activation(
+                out=squares[:], in_=o_bank[:], func=ACT.Square, accum_out=o_squares[:, b : b + 1]
+            )
+
+        for b in range(BLOCKS + 1):
+            if b + 2 < BLOCKS:
+                down_squares(b + 2)
+            if b + 1 < BLOCKS:
+                down_factors(b + 1)
+            if b < BLOCKS:
+                down_scale(b)
+            if b > 0:
+                down_product(b - 1)
+
+        o_total = small.tile([P, 1], F32, tag="o_total")
+        nc.vector.tensor_reduce(out=o_total[:], in_=o_squares[:], axis=AX.X, op=ALU.add)
+        o_inverse = one_over_norm(o_total[:], 1)
+        out_view = out.rearrange("b l d -> b (l d)")
+        STORE = 1024
+        for s in range(D_MODEL // STORE):
+            cols = o_cols(s * STORE, STORE)
+            nc.vector.tensor_scalar_mul(out=cols, in0=cols, scalar1=o_inverse[:, 0:1])
+            nc.sync.dma_start(out=out_view[:, s * STORE : (s + 1) * STORE], in_=cols)

@@ -25,7 +25,15 @@ PAIRS = 2 * P
 BANK = 512
 D_LOAD = 2048
 NORM_FLOOR = 1e-12
-GPSIMD_EVERY = 3
+GU_TILES = 4 * (PASSES // CHUNK)
+BLOCKS = D_MODEL // BANK
+TILES = GU_TILES + BLOCKS
+GU_STEPS = 4 * PASSES
+STEPS = GU_STEPS + 2 * BLOCKS
+STEPS_AHEAD = PASSES + 3
+STEPS_PER_TILE = 5
+SPREAD_LAG = 3
+STORE = 1024
 
 FLOPS = 3 * 2 * TOKENS * D_MODEL * HIDDEN
 
@@ -34,14 +42,15 @@ def tile_npertokenswishglu_k_kernel(tc, x, W_gate, W_up, W_down, s_u, s_v, out):
     nc = tc.nc
     with ExitStack() as ctx:
         const = ctx.enter_context(tc.tile_pool(name="const", bufs=1))
-        big = ctx.enter_context(tc.tile_pool(name="big", bufs=8))
-        factor_pool = ctx.enter_context(tc.tile_pool(name="factor_pool", bufs=3))
+        big = ctx.enter_context(tc.tile_pool(name="big", bufs=9))
         work = ctx.enter_context(tc.tile_pool(name="work", bufs=3))
+        packed = ctx.enter_context(tc.tile_pool(name="packed", bufs=4))
         junk = ctx.enter_context(tc.tile_pool(name="junk", bufs=4))
         small = ctx.enter_context(tc.tile_pool(name="small", bufs=4))
         turned_pool = ctx.enter_context(tc.psum_pool(name="turned_pool", bufs=3))
-        spread_pool = ctx.enter_context(tc.psum_pool(name="spread_pool", bufs=3))
-        acc_pool = ctx.enter_context(tc.psum_pool(name="acc_pool", bufs=2))
+        spread_pool = ctx.enter_context(tc.psum_pool(name="spread_pool", bufs=2))
+        acc_pool = ctx.enter_context(tc.psum_pool(name="acc_pool", bufs=3))
+        ctx.enter_context(tc.manual_schedule())
 
         ident = const.tile([P, P], F32, tag="ident")
         make_identity(nc, ident[:])
@@ -49,61 +58,19 @@ def tile_npertokenswishglu_k_kernel(tc, x, W_gate, W_up, W_down, s_u, s_v, out):
         make_identity(nc, ident_bf[:])
         minus_half = const.tile([P, 4], F32, tag="minus_half")
         nc.vector.memset(minus_half[:], -0.5)
-
-        def add_up_squares(bank, sums):
-            halves = bank[:].bitcast(BF16).rearrange("q (k e) -> q k e", e=2)
-            for e in range(2):
-                squares = junk.tile([P, BANK], BF16, tag="squares")
-                nc.scalar.activation(
-                    out=squares[:], in_=halves[:, :, e], func=ACT.Square, accum_out=sums[e]
-                )
-
-        def one_over_norm(sum_of_squares, width):
-            floored = small.tile([P, width], F32, tag="floored")
-            nc.gpsimd.tensor_scalar_max(
-                out=floored[:], in0=sum_of_squares, scalar1=NORM_FLOOR * NORM_FLOOR
-            )
-            inverse = small.tile([P, width], F32, tag="inverse")
-            nc.gpsimd.tensor_tensor(
-                out=inverse[:], in0=floored[:], in1=minus_half[:, 0:width], op=ALU.pow
-            )
-            return inverse
-
-        def spread_over_partitions(inverse, width):
-            spread = spread_pool.tile([P, width, P], F32, tag="spread")
-            for c in range(width):
-                nc.tensor.transpose(
-                    spread[:, c, :], inverse[:, c : c + 1].to_broadcast([P, P]), ident[:]
-                )
-            return spread
-
-        def for_gpsimd(group):
-            return group % GPSIMD_EVERY == GPSIMD_EVERY - 1
-
-        def copy_for_gpsimd(spread_pair):
-            factors = factor_pool.tile([P, 2, P], F32, tag="factors")
-            nc.vector.tensor_copy(out=factors[:], in_=spread_pair)
-            return factors
-
-        def scale_and_group(engine, grouped_cols, raw_rows, spread_pair):
-            engine.tensor_tensor(
-                out=grouped_cols.rearrange("p (q e j) -> p q e j", e=2, j=PACK),
-                in0=raw_rows.rearrange("p j (q e) -> p q e j", e=2),
-                in1=spread_pair.rearrange("p e q -> p q e")
-                .unsqueeze(3)
-                .to_broadcast([P, P, 2, PACK]),
-                op=ALU.mult,
-            )
-
         gain_rows = const.tile([P, P], BF16, tag="gain_rows")
         nc.vector.memset(gain_rows[:], 0.0)
         nc.scalar.dma_start(out=gain_rows[0:4, :], in_=s_u.rearrange("o (t c) -> (o t) c", c=P))
         nc.scalar.dma_start(out=gain_rows[4:8, :], in_=s_v.rearrange("o (t c) -> (o t) c", c=P))
 
-        gate_view = W_gate.rearrange("l (g p j) f -> p (l g) (j f)", p=P, j=PACK)
-        up_view = W_up.rearrange("l (g p j) f -> p (l g) (j f)", p=P, j=PACK)
+        x_view = x.rearrange("b l d -> b (l d)")
+        x_raw = big.tile([P, D_MODEL], BF16, tag="big")
+        for c in range(PASSES // CHUNK):
+            cols = slice(c * CHUNK * K_PASS, (c + 1) * CHUNK * K_PASS)
+            nc.sync.dma_start(out=x_raw[:, cols], in_=x_view[:, cols])
 
-        def load_gate_or_up(view, c):
+        def load_gate_or_up(weight, c):
+            view = weight.rearrange("l (g p j) f -> p (l g) (j f)", p=P, j=PACK)
             raw = big.tile([P, CHUNK, PACK, HIDDEN], BF16, tag="big")
             for i in range(CHUNK):
                 nc.sync.dma_start(
@@ -111,15 +78,20 @@ def tile_npertokenswishglu_k_kernel(tc, x, W_gate, W_up, W_down, s_u, s_v, out):
                 )
             return raw
 
-        gate_raw = [load_gate_or_up(gate_view, c) for c in range(PASSES // CHUNK)]
-        x_raw = const.tile([P, D_MODEL], BF16, tag="x_raw")
-        nc.sync.dma_start(out=x_raw[:], in_=x.rearrange("b l d -> b (l d)"))
-        up_raw = [load_gate_or_up(up_view, c) for c in range(PASSES // CHUNK)]
+        gate_raw = [load_gate_or_up(W_gate, c) for c in range(PASSES // CHUNK)]
+        up_raw = [load_gate_or_up(W_up, c) for c in range(PASSES // CHUNK)]
+        down_raw = []
+
+        def load_down(c):
+            view = W_down.rearrange("l (t p) d -> p (l t) d", p=P)
+            raw = big.tile([P, PACK, D_LOAD], BF16, tag="big")
+            nc.sync.dma_start(out=raw[:], in_=view[:, :, c * D_LOAD : (c + 1) * D_LOAD])
+            down_raw.append(raw)
+
         x_words = x_raw[:].bitcast(F32).rearrange("b (g p u) -> b g u p", p=P, u=2)
         x_codes = const.tile([P, PASSES, TOKENS], U32, tag="x_codes", align_bytes=64)
         x_plane = const.tile([P, PASSES, TOKENS], U8, tag="x_plane", align_bytes=64)
-
-        def quantise_x(c):
+        for c in range(PASSES // CHUNK):
             x_grouped = work.tile([P, CHUNK, TOKENS * PACK], BF16, tag="grouped", align_bytes=64)
             x_grouped_words = x_grouped[:].bitcast(F32)
             for h in range(2):
@@ -136,207 +108,218 @@ def tile_npertokenswishglu_k_kernel(tc, x, W_gate, W_up, W_down, s_u, s_v, out):
                     ),
                     in_=bank[:].rearrange("p (i u b) -> p i b u", i=2, u=2),
                 )
+            passes = slice(c * CHUNK, (c + 1) * CHUNK)
             nc.vector.quantize_mx(
-                out=x_codes[:, c * CHUNK : (c + 1) * CHUNK, :]
-                .rearrange("p g b -> p (g b)")
-                .bitcast(FP8X4),
-                scales=x_plane[:, c * CHUNK : (c + 1) * CHUNK, :].rearrange("p g b -> p (g b)"),
+                out=x_codes[:, passes, :].rearrange("p g b -> p (g b)").bitcast(FP8X4),
+                scales=x_plane[:, passes, :].rearrange("p g b -> p (g b)"),
                 in_=x_grouped[:].rearrange("p g n -> p (g n)"),
             )
+        load_down(0)
 
-        def prepare_gains():
-            gain_cols = turned_pool.tile([P, P], BF16, tag="turned")
-            nc.tensor.transpose(gain_cols[:], gain_rows[:], ident_bf[:])
-            gains = const.tile([P, 8], F32, tag="gains")
-            nc.vector.tensor_copy(out=gains[:], in_=gain_cols[:, 0:8])
-            nc.vector.scalar_tensor_tensor(
-                out=sizes[:], in0=gains[:], scalar=-1.0, in1=gains[:], op0=ALU.mult, op1=ALU.max
-            )
-            nc.vector.tensor_scalar_mul(
-                out=sizes[:, 4:8], in0=sizes[:, 4:8], scalar1=math.sqrt(float(D_MODEL))
-            )
-
+        gain_cols = turned_pool.tile([P, P], BF16, tag="turned")
+        nc.tensor.transpose(gain_cols[:], gain_rows[:], ident_bf[:])
+        gains = const.tile([P, 8], F32, tag="gains")
+        nc.vector.tensor_copy(out=gains[:], in_=gain_cols[:, 0:8])
         sizes = const.tile([P, 8], F32, tag="sizes")
+        nc.vector.scalar_tensor_tensor(
+            out=sizes[:], in0=gains[:], scalar=-1.0, in1=gains[:], op0=ALU.mult, op1=ALU.max
+        )
+        nc.vector.tensor_scalar_mul(
+            out=sizes[:, 4:8], in0=sizes[:, 4:8], scalar1=math.sqrt(float(D_MODEL))
+        )
 
-        def gate_up_norms(raw, half):
-            sums = small.tile([P, 2, PASSES], F32, tag="sums")
-            for g in range(PASSES):
-                words = raw[g // CHUNK][:, g % CHUNK, :, :].bitcast(F32)
-                bank = turned_pool.tile([P, BANK], F32, tag="turned")
+        def add_up_squares(bank, sums):
+            halves = bank[:].bitcast(BF16).rearrange("q (k e) -> q k e", e=2)
+            for e in range(2):
+                squares = junk.tile([P, BANK], BF16, tag="squares")
+                nc.scalar.activation(
+                    out=squares[:], in_=halves[:, :, e], func=ACT.Square, accum_out=sums[e]
+                )
+
+        def one_over_norm(inverse, sum_of_squares, width):
+            floored = small.tile([P, width], F32, tag="floored")
+            nc.gpsimd.tensor_scalar_max(
+                out=floored[:], in0=sum_of_squares, scalar1=NORM_FLOOR * NORM_FLOOR
+            )
+            nc.gpsimd.tensor_tensor(
+                out=inverse, in0=floored[:], in1=minus_half[:, 0:width], op=ALU.pow
+            )
+
+        def spread_over_partitions(inverse, width):
+            spread = spread_pool.tile([P, width, P], F32, tag="spread")
+            for c in range(width):
+                nc.tensor.transpose(
+                    spread[:, c, :], inverse[:, c : c + 1].to_broadcast([P, P]), ident[:]
+                )
+            return spread
+
+        gu_raw = [gate_raw, gate_raw, up_raw, up_raw]
+        gu_sums = [None] * 4
+        gu_inverse = const.tile([P, 4, 2], F32, tag="gu_inverse")
+        gu_spread = [None] * 4
+        down_inverse = const.tile([P, BLOCKS, 4], F32, tag="down_inverse")
+        down_sums = [None] * BLOCKS
+        down_spread = [None] * BLOCKS
+
+        def down_rows(b, unit):
+            first = (b % (D_LOAD // BANK)) * BANK + unit * PAIRS
+            return down_raw[b // (D_LOAD // BANK)][:, :, first : first + PAIRS]
+
+        def squares_step(s):
+            bank = turned_pool.tile([P, BANK], F32, tag="turned")
+            if s < GU_STEPS:
+                job, g = s // PASSES, s % PASSES
+                half = job % 2
+                if g == 0:
+                    gu_sums[job] = small.tile([P, 2, PASSES], F32, tag="gu_sums", name="gu_sums")
+                words = gu_raw[job][g // CHUNK][:, g % CHUNK, :, :].bitcast(F32)
                 for j in range(PACK):
                     nc.tensor.transpose(
                         bank[:, j * P : (j + 1) * P], words[:, j, half * P : (half + 1) * P], ident[:]
                     )
-                add_up_squares(bank, [sums[:, e, g : g + 1] for e in range(2)])
-            total = small.tile([P, 2], F32, tag="total")
-            nc.vector.tensor_reduce(out=total[:], in_=sums[:], axis=AX.X, op=ALU.add)
-            return spread_over_partitions(one_over_norm(total[:], 2), 2)
-
-        def gate_up_products(raw, half, spread):
-            acc = [acc_pool.tile([P, TOKENS], F32, tag="acc", name="acc%d" % m) for m in range(2)]
-            grouped = [None] * (PASSES // CHUNK)
-            factors = copy_for_gpsimd(spread[:])
-
-            def scale(c):
-                grouped[c] = work.tile(
-                    [P, CHUNK, PAIRS * PACK], BF16, tag="grouped", align_bytes=64, name="grouped"
-                )
-                for i in range(CHUNK):
-                    on_gpsimd = for_gpsimd(c * CHUNK + i)
-                    scale_and_group(
-                        nc.gpsimd if on_gpsimd else nc.vector,
-                        grouped[c][:, i, :],
-                        raw[c][:, i, :, half * PAIRS : (half + 1) * PAIRS],
-                        factors[:] if on_gpsimd else spread[:],
-                    )
-
-            def quantise_and_multiply(c):
-                codes = work.tile([P, CHUNK, PAIRS], U32, tag="codes", align_bytes=64)
-                plane = work.tile([P, CHUNK, PAIRS], U8, tag="plane", align_bytes=64)
-                nc.vector.quantize_mx(
-                    out=codes[:].rearrange("p g w -> p (g w)").bitcast(FP8X4),
-                    scales=plane[:].rearrange("p g w -> p (g w)"),
-                    in_=grouped[c][:].rearrange("p g n -> p (g n)"),
-                )
-                for m in range(2):
-                    for i in range(CHUNK):
-                        g = c * CHUNK + i
-                        nc.tensor.matmul_mx(
-                            out=acc[m][:],
-                            lhsT=codes[:, i, m * P : (m + 1) * P].bitcast(FP8X4),
-                            lhsT_scale=plane[:, i, m * P : (m + 1) * P],
-                            rhs=x_codes[:, g, :].bitcast(FP8X4),
-                            rhs_scale=x_plane[:, g, :],
-                            start=(g == 0),
-                            stop=(g == PASSES - 1),
+                add_up_squares(bank, [gu_sums[job][:, e, g : g + 1] for e in range(2)])
+                if g == PASSES - 1:
+                    total = small.tile([P, 2], F32, tag="total")
+                    for e in range(2):
+                        copied = small.tile([P, PASSES], F32, tag="copied")
+                        nc.scalar.activation(
+                            out=copied[:],
+                            in_=gu_sums[job][:, e, :],
+                            func=ACT.Copy,
+                            accum_out=total[:, e : e + 1],
                         )
-
-            scale(0)
-            for c in range(1, PASSES // CHUNK):
-                scale(c)
-                quantise_and_multiply(c - 1)
-            quantise_and_multiply(PASSES // CHUNK - 1)
-            return acc
-
-        u_scaled = const.tile([P, PACK, TOKENS], F32, tag="u_scaled")
-        h_grouped = const.tile([P, TOKENS, PACK], BF16, tag="h_grouped", align_bytes=64)
-
-        def keep_gate(half, acc):
-            for m in range(2):
-                t = 2 * half + m
-                nc.scalar.activation(
-                    out=u_scaled[:, t, :], in_=acc[m][:], func=ACT.Copy, scale=sizes[:, t : t + 1]
-                )
-
-        def make_hidden(half, acc):
-            for m in range(2):
-                t = 2 * half + m
-                swish = small.tile([P, TOKENS], F32, tag="swish")
-                nc.scalar.activation(
-                    out=swish[:], in_=acc[m][:], func=ACT.Silu, scale=sizes[:, 4 + t : 5 + t]
-                )
-                nc.vector.tensor_tensor(
-                    out=h_grouped[:, :, t], in0=swish[:], in1=u_scaled[:, t, :], op=ALU.mult
-                )
-
-        gate_spread_0 = gate_up_norms(gate_raw, 0)
-        for c in range(PASSES // CHUNK):
-            quantise_x(c)
-        prepare_gains()
-        gate_spread_1 = gate_up_norms(gate_raw, 1)
-        keep_gate(0, gate_up_products(gate_raw, 0, gate_spread_0))
-        up_spread_0 = gate_up_norms(up_raw, 0)
-        keep_gate(1, gate_up_products(gate_raw, 1, gate_spread_1))
-
-        down_view = W_down.rearrange("l (t p) d -> p (l t) d", p=P)
-        down_raw = []
-        for c in range(D_MODEL // D_LOAD):
-            raw = big.tile([P, PACK, D_LOAD], BF16, tag="big", name="down_raw")
-            nc.sync.dma_start(out=raw[:], in_=down_view[:, :, c * D_LOAD : (c + 1) * D_LOAD])
-            down_raw.append(raw)
-
-        BLOCKS = D_MODEL // BANK
-        PER_LOAD = D_LOAD // BANK
-        down_sums = [None] * BLOCKS
-        down_spread = [None] * BLOCKS
-        down_grouped = [None] * BLOCKS
-        down_factors_sb = [None] * (2 * BLOCKS)
-
-        def down_rows(b, unit):
-            first = (b % PER_LOAD) * BANK + unit * PAIRS
-            return down_raw[b // PER_LOAD][:, :, first : first + PAIRS]
-
-        def down_squares(b):
-            down_sums[b] = small.tile([P, 4], F32, tag="down_sums", name="down_sums")
-            for unit in range(2):
+                    one_over_norm(gu_inverse[:, job, :], total[:], 2)
+            else:
+                b, unit = (s - GU_STEPS) // 2, (s - GU_STEPS) % 2
+                if unit == 0:
+                    down_sums[b] = small.tile([P, 4], F32, tag="down_sums", name="down_sums")
                 words = down_rows(b, unit).bitcast(F32)
-                bank = turned_pool.tile([P, BANK], F32, tag="turned")
                 for t in range(PACK):
                     nc.tensor.transpose(bank[:, t * P : (t + 1) * P], words[:, t, :], ident[:])
                 add_up_squares(
                     bank, [down_sums[b][:, 2 * unit + e : 2 * unit + e + 1] for e in range(2)]
                 )
+                if unit == 1:
+                    one_over_norm(down_inverse[:, b, :], down_sums[b][:], 4)
+            if s >= PASSES + SPREAD_LAG - 1 and (s - SPREAD_LAG + 1) % PASSES == 0 and s < GU_STEPS + PASSES:
+                job = (s - SPREAD_LAG + 1) // PASSES - 1
+                gu_spread[job] = spread_over_partitions(gu_inverse[:, job, :], 2)
 
-        def down_factors(b):
-            down_spread[b] = spread_over_partitions(one_over_norm(down_sums[b][:], 4), 4)
-            for unit in range(2):
-                if for_gpsimd(2 * b + unit):
-                    down_factors_sb[2 * b + unit] = copy_for_gpsimd(
-                        down_spread[b][:, 2 * unit : 2 * unit + 2, :]
-                    )
-
-        def down_scale(b):
-            down_grouped[b] = work.tile(
-                [P, 2, PAIRS * PACK], BF16, tag="grouped", align_bytes=64, name="down_grouped"
+        def scale_and_group(grouped_cols, raw_rows, spread_pair):
+            nc.vector.tensor_tensor(
+                out=grouped_cols.rearrange("p (q e j) -> p q e j", e=2, j=PACK),
+                in0=raw_rows.rearrange("p j (q e) -> p q e j", e=2),
+                in1=spread_pair.rearrange("p e q -> p q e")
+                .unsqueeze(3)
+                .to_broadcast([P, P, 2, PACK]),
+                op=ALU.mult,
             )
-            for unit in range(2):
-                on_gpsimd = for_gpsimd(2 * b + unit)
-                scale_and_group(
-                    nc.gpsimd if on_gpsimd else nc.vector,
-                    down_grouped[b][:, unit, :],
-                    down_rows(b, unit),
-                    down_factors_sb[2 * b + unit][:]
-                    if on_gpsimd
-                    else down_spread[b][:, 2 * unit : 2 * unit + 2, :],
-                )
 
-        up_spread_1 = gate_up_norms(up_raw, 1)
-        make_hidden(0, gate_up_products(up_raw, 0, up_spread_0))
-        down_squares(0)
-        down_squares(1)
-        down_factors(0)
-        make_hidden(1, gate_up_products(up_raw, 1, up_spread_1))
-
+        grouped = [None] * TILES
+        codes = [None] * TILES
+        plane = [None] * TILES
+        acc = [None] * 4
+        u_scaled = const.tile([P, PACK, TOKENS], F32, tag="u_scaled")
+        h_grouped = const.tile([P, TOKENS, PACK], BF16, tag="h_grouped", align_bytes=64)
         h_codes = const.tile([P, TOKENS], U32, tag="h_codes", align_bytes=64)
         h_plane = const.tile([P, TOKENS], U8, tag="h_plane", align_bytes=64)
-        nc.vector.quantize_mx(
-            out=h_codes[:].bitcast(FP8X4),
-            scales=h_plane[:],
-            in_=h_grouped[:].rearrange("p b t -> p (b t)"),
-        )
-
-        O_HALF = D_MODEL // 2
-        o_sb = [big.tile([P, O_HALF], F32, tag="big", name="o_sb%d" % i) for i in range(2)]
+        o_sb = []
         o_squares = const.tile([P, BLOCKS], F32, tag="o_squares")
 
         def o_cols(first, width):
-            return o_sb[first // O_HALF][:, first % O_HALF : first % O_HALF + width]
+            half = D_MODEL // 2
+            return o_sb[first // half][:, first % half : first % half + width]
 
-        def down_product(b):
-            codes = work.tile([P, BANK], U32, tag="codes", align_bytes=64)
-            plane = work.tile([P, BANK], U8, tag="plane", align_bytes=64)
-            nc.vector.quantize_mx(
-                out=codes[:].bitcast(FP8X4),
-                scales=plane[:],
-                in_=down_grouped[b][:].rearrange("p u n -> p (u n)"),
+        def scale(v):
+            grouped[v] = work.tile(
+                [P, CHUNK * PAIRS * PACK], BF16, tag="grouped", align_bytes=64, name="grouped"
             )
+            n = PAIRS * PACK
+            if v < GU_TILES:
+                job, c = v // (PASSES // CHUNK), v % (PASSES // CHUNK)
+                half = job % 2
+                for i in range(CHUNK):
+                    scale_and_group(
+                        grouped[v][:, i * n : (i + 1) * n],
+                        gu_raw[job][c][:, i, :, half * PAIRS : (half + 1) * PAIRS],
+                        gu_spread[job][:],
+                    )
+            else:
+                b = v - GU_TILES
+                for unit in range(2):
+                    scale_and_group(
+                        grouped[v][:, unit * n : (unit + 1) * n],
+                        down_rows(b, unit),
+                        down_spread[b][:, 2 * unit : 2 * unit + 2, :],
+                    )
+
+        def quantise(v):
+            words = CHUNK * PAIRS if v < GU_TILES else BANK
+            codes[v] = packed.tile([P, CHUNK * PAIRS], U32, tag="codes", align_bytes=64, name="codes")
+            plane[v] = packed.tile([P, CHUNK * PAIRS], U8, tag="plane", align_bytes=64, name="plane")
+            nc.vector.quantize_mx(
+                out=codes[v][:, 0:words].bitcast(FP8X4),
+                scales=plane[v][:, 0:words],
+                in_=grouped[v][:, 0 : words * PACK],
+            )
+
+        def multiply_gate_up(v):
+            job, c = v // (PASSES // CHUNK), v % (PASSES // CHUNK)
+            if c == 0:
+                acc[job] = [
+                    acc_pool.tile([P, TOKENS], F32, tag="acc", name="acc%d" % m) for m in range(2)
+                ]
+            for m in range(2):
+                for i in range(CHUNK):
+                    g = c * CHUNK + i
+                    cols = slice(i * PAIRS + m * P, i * PAIRS + (m + 1) * P)
+                    nc.tensor.matmul_mx(
+                        out=acc[job][m][:],
+                        lhsT=codes[v][:, cols].bitcast(FP8X4),
+                        lhsT_scale=plane[v][:, cols],
+                        rhs=x_codes[:, g, :].bitcast(FP8X4),
+                        rhs_scale=x_plane[:, g, :],
+                        start=(g == 0),
+                        stop=(g == PASSES - 1),
+                    )
+            if c < PASSES // CHUNK - 1:
+                return
+            for m in range(2):
+                t = 2 * (job % 2) + m
+                if job < 2:
+                    nc.scalar.activation(
+                        out=u_scaled[:, t, :],
+                        in_=acc[job][m][:],
+                        func=ACT.Copy,
+                        scale=sizes[:, t : t + 1],
+                    )
+                else:
+                    swish = small.tile([P, TOKENS], F32, tag="swish")
+                    nc.scalar.activation(
+                        out=swish[:], in_=acc[job][m][:], func=ACT.Silu, scale=sizes[:, 4 + t : 5 + t]
+                    )
+                    nc.vector.tensor_tensor(
+                        out=h_grouped[:, :, t], in0=swish[:], in1=u_scaled[:, t, :], op=ALU.mult
+                    )
+            if job == 3:
+                nc.vector.quantize_mx(
+                    out=h_codes[:].bitcast(FP8X4),
+                    scales=h_plane[:],
+                    in_=h_grouped[:].rearrange("p b t -> p (b t)"),
+                )
+
+        def multiply_down(v):
+            b = v - GU_TILES
+            if b == 0:
+                for i in range(2):
+                    o_sb.append(big.tile([P, D_MODEL // 2], F32, tag="big", name="o_sb%d" % i))
             o_bank = acc_pool.tile([P, BANK], F32, tag="acc")
             nc.tensor.matmul_mx(
                 out=o_bank[:],
                 lhsT=h_codes[:].bitcast(FP8X4),
                 lhsT_scale=h_plane[:],
-                rhs=codes[:].bitcast(FP8X4),
-                rhs_scale=plane[:],
+                rhs=codes[v][:, 0:BANK].bitcast(FP8X4),
+                rhs_scale=plane[v][:, 0:BANK],
                 start=True,
                 stop=True,
             )
@@ -346,21 +329,33 @@ def tile_npertokenswishglu_k_kernel(tc, x, W_gate, W_up, W_down, s_u, s_v, out):
                 out=squares[:], in_=o_bank[:], func=ACT.Square, accum_out=o_squares[:, b : b + 1]
             )
 
-        for b in range(BLOCKS + 1):
-            if b + 2 < BLOCKS:
-                down_squares(b + 2)
-            if b + 1 < BLOCKS:
-                down_factors(b + 1)
-            if b < BLOCKS:
-                down_scale(b)
-            if b > 0:
-                down_product(b - 1)
+        for s in range(STEPS_AHEAD):
+            squares_step(s)
+        for v in range(TILES + 2):
+            first = STEPS_AHEAD + v * STEPS_PER_TILE
+            for s in range(min(first, STEPS), min(first + STEPS_PER_TILE, STEPS)):
+                squares_step(s)
+            if v == 2 * (PASSES // CHUNK):
+                for c in range(1, D_MODEL // D_LOAD):
+                    load_down(c)
+            if GU_TILES <= v + 1 < TILES:
+                b = v + 1 - GU_TILES
+                down_spread[b] = spread_over_partitions(down_inverse[:, b, :], 4)
+            if v < TILES:
+                scale(v)
+            if 1 <= v <= TILES:
+                quantise(v - 1)
+            if 2 <= v and v - 2 < GU_TILES:
+                multiply_gate_up(v - 2)
+            if v - 2 >= GU_TILES:
+                multiply_down(v - 2)
 
         o_total = small.tile([P, 1], F32, tag="o_total")
-        nc.vector.tensor_reduce(out=o_total[:], in_=o_squares[:], axis=AX.X, op=ALU.add)
-        o_inverse = one_over_norm(o_total[:], 1)
+        copied = small.tile([P, BLOCKS], F32, tag="copied")
+        nc.scalar.activation(out=copied[:], in_=o_squares[:], func=ACT.Copy, accum_out=o_total[:])
+        o_inverse = small.tile([P, 1], F32, tag="o_inverse")
+        one_over_norm(o_inverse[:], o_total[:], 1)
         out_view = out.rearrange("b l d -> b (l d)")
-        STORE = 1024
         for s in range(D_MODEL // STORE):
             cols = o_cols(s * STORE, STORE)
             nc.vector.tensor_scalar_mul(out=cols, in0=cols, scalar1=o_inverse[:, 0:1])

@@ -31,7 +31,8 @@ TILES = GU_TILES + BLOCKS
 GU_STEPS = 4 * PASSES
 STEPS = GU_STEPS + 2 * BLOCKS
 STEPS_AHEAD = PASSES + 3
-STEPS_PER_TILE = 5
+STEPS_PER_TILE = 4
+GPSIMD_EVERY = 4
 SPREAD_LAG = 3
 STORE = 1024
 
@@ -47,6 +48,7 @@ def tile_npertokenswishglu_k_kernel(tc, x, W_gate, W_up, W_down, s_u, s_v, out):
         packed = ctx.enter_context(tc.tile_pool(name="packed", bufs=4))
         junk = ctx.enter_context(tc.tile_pool(name="junk", bufs=4))
         small = ctx.enter_context(tc.tile_pool(name="small", bufs=4))
+        factor_pool = ctx.enter_context(tc.tile_pool(name="factor_pool", bufs=3))
         turned_pool = ctx.enter_context(tc.psum_pool(name="turned_pool", bufs=3))
         spread_pool = ctx.enter_context(tc.psum_pool(name="spread_pool", bufs=2))
         acc_pool = ctx.enter_context(tc.psum_pool(name="acc_pool", bufs=3))
@@ -205,8 +207,13 @@ def tile_npertokenswishglu_k_kernel(tc, x, W_gate, W_up, W_down, s_u, s_v, out):
                 job = (s - SPREAD_LAG + 1) // PASSES - 1
                 gu_spread[job] = spread_over_partitions(gu_inverse[:, job, :], 2)
 
-        def scale_and_group(grouped_cols, raw_rows, spread_pair):
-            nc.vector.tensor_tensor(
+        def copy_for_gpsimd(spread_pair):
+            factors = factor_pool.tile([P, 2, P], F32, tag="factors")
+            nc.vector.tensor_copy(out=factors[:], in_=spread_pair)
+            return factors
+
+        def scale_and_group(engine, grouped_cols, raw_rows, spread_pair):
+            engine.tensor_tensor(
                 out=grouped_cols.rearrange("p (q e j) -> p q e j", e=2, j=PACK),
                 in0=raw_rows.rearrange("p j (q e) -> p q e j", e=2),
                 in1=spread_pair.rearrange("p e q -> p q e")
@@ -219,6 +226,7 @@ def tile_npertokenswishglu_k_kernel(tc, x, W_gate, W_up, W_down, s_u, s_v, out):
         codes = [None] * TILES
         plane = [None] * TILES
         acc = [None] * 4
+        gu_factors = [None] * 4
         u_scaled = const.tile([P, PACK, TOKENS], F32, tag="u_scaled")
         h_grouped = const.tile([P, TOKENS, PACK], BF16, tag="h_grouped", align_bytes=64)
         h_codes = const.tile([P, TOKENS], U32, tag="h_codes", align_bytes=64)
@@ -238,19 +246,26 @@ def tile_npertokenswishglu_k_kernel(tc, x, W_gate, W_up, W_down, s_u, s_v, out):
             if v < GU_TILES:
                 job, c = v // (PASSES // CHUNK), v % (PASSES // CHUNK)
                 half = job % 2
-                for i in range(CHUNK):
+                if c == 0:
+                    gu_factors[job] = copy_for_gpsimd(gu_spread[job][:])
+                for i in reversed(range(CHUNK)):
+                    on_gpsimd = i % GPSIMD_EVERY == GPSIMD_EVERY - 1
                     scale_and_group(
+                        nc.gpsimd if on_gpsimd else nc.vector,
                         grouped[v][:, i * n : (i + 1) * n],
                         gu_raw[job][c][:, i, :, half * PAIRS : (half + 1) * PAIRS],
-                        gu_spread[job][:],
+                        gu_factors[job][:] if on_gpsimd else gu_spread[job][:],
                     )
             else:
                 b = v - GU_TILES
-                for unit in range(2):
+                for unit in reversed(range(2)):
+                    on_gpsimd = (2 * b + unit) % GPSIMD_EVERY == GPSIMD_EVERY - 1
+                    spread_pair = down_spread[b][:, 2 * unit : 2 * unit + 2, :]
                     scale_and_group(
+                        nc.gpsimd if on_gpsimd else nc.vector,
                         grouped[v][:, unit * n : (unit + 1) * n],
                         down_rows(b, unit),
-                        down_spread[b][:, 2 * unit : 2 * unit + 2, :],
+                        copy_for_gpsimd(spread_pair)[:] if on_gpsimd else spread_pair,
                     )
 
         def quantise(v):

@@ -32,7 +32,6 @@ GU_STEPS = 4 * PASSES
 STEPS = GU_STEPS + 2 * BLOCKS
 STEPS_AHEAD = PASSES + 3
 STEPS_PER_TILE = 4
-GPSIMD_EVERY = 4
 SPREAD_LAG = 3
 STORE = 1024
 
@@ -48,7 +47,6 @@ def tile_npertokenswishglu_k_kernel(tc, x, W_gate, W_up, W_down, s_u, s_v, out):
         packed = ctx.enter_context(tc.tile_pool(name="packed", bufs=4))
         junk = ctx.enter_context(tc.tile_pool(name="junk", bufs=4))
         small = ctx.enter_context(tc.tile_pool(name="small", bufs=4))
-        factor_pool = ctx.enter_context(tc.tile_pool(name="factor_pool", bufs=3))
         turned_pool = ctx.enter_context(tc.psum_pool(name="turned_pool", bufs=3))
         spread_pool = ctx.enter_context(tc.psum_pool(name="spread_pool", bufs=2))
         acc_pool = ctx.enter_context(tc.psum_pool(name="acc_pool", bufs=3))
@@ -147,12 +145,15 @@ def tile_npertokenswishglu_k_kernel(tc, x, W_gate, W_up, W_down, s_u, s_v, out):
                 out=inverse, in0=floored[:], in1=minus_half[:, 0:width], op=ALU.pow
             )
 
-        def spread_over_partitions(inverse, width):
-            spread = spread_pool.tile([P, width, P], F32, tag="spread")
-            for c in range(width):
-                nc.tensor.transpose(
-                    spread[:, c, :], inverse[:, c : c + 1].to_broadcast([P, P]), ident[:]
-                )
+        def spread_over_partitions(inverse, groups):
+            spread = spread_pool.tile([P, groups * PAIRS], F32, tag="spread")
+            by_half = spread[:].rearrange("p (n q e) -> p n e q", q=P, e=2)
+            for n in range(groups):
+                for e in range(2):
+                    c = 2 * n + e
+                    nc.tensor.transpose(
+                        by_half[:, n, e, :], inverse[:, c : c + 1].to_broadcast([P, P]), ident[:]
+                    )
             return spread
 
         gu_raw = [gate_raw, gate_raw, up_raw, up_raw]
@@ -205,28 +206,12 @@ def tile_npertokenswishglu_k_kernel(tc, x, W_gate, W_up, W_down, s_u, s_v, out):
                     one_over_norm(down_inverse[:, b, :], down_sums[b][:], 4)
             if s >= PASSES + SPREAD_LAG - 1 and (s - SPREAD_LAG + 1) % PASSES == 0 and s < GU_STEPS + PASSES:
                 job = (s - SPREAD_LAG + 1) // PASSES - 1
-                gu_spread[job] = spread_over_partitions(gu_inverse[:, job, :], 2)
-
-        def copy_for_gpsimd(spread_pair):
-            factors = factor_pool.tile([P, 2, P], F32, tag="factors")
-            nc.vector.tensor_copy(out=factors[:], in_=spread_pair)
-            return factors
-
-        def scale_and_group(engine, grouped_cols, raw_rows, spread_pair):
-            engine.tensor_tensor(
-                out=grouped_cols.rearrange("p (q e j) -> p q e j", e=2, j=PACK),
-                in0=raw_rows.rearrange("p j (q e) -> p q e j", e=2),
-                in1=spread_pair.rearrange("p e q -> p q e")
-                .unsqueeze(3)
-                .to_broadcast([P, P, 2, PACK]),
-                op=ALU.mult,
-            )
+                gu_spread[job] = spread_over_partitions(gu_inverse[:, job, :], 1)
 
         grouped = [None] * TILES
         codes = [None] * TILES
         plane = [None] * TILES
         acc = [None] * 4
-        gu_factors = [None] * 4
         u_scaled = const.tile([P, PACK, TOKENS], F32, tag="u_scaled")
         h_grouped = const.tile([P, TOKENS, PACK], BF16, tag="h_grouped", align_bytes=64)
         h_codes = const.tile([P, TOKENS], U32, tag="h_codes", align_bytes=64)
@@ -242,31 +227,31 @@ def tile_npertokenswishglu_k_kernel(tc, x, W_gate, W_up, W_down, s_u, s_v, out):
             grouped[v] = work.tile(
                 [P, CHUNK * PAIRS * PACK], BF16, tag="grouped", align_bytes=64, name="grouped"
             )
-            n = PAIRS * PACK
             if v < GU_TILES:
                 job, c = v // (PASSES // CHUNK), v % (PASSES // CHUNK)
                 half = job % 2
-                if c == 0:
-                    gu_factors[job] = copy_for_gpsimd(gu_spread[job][:])
-                for i in reversed(range(CHUNK)):
-                    on_gpsimd = i % GPSIMD_EVERY == GPSIMD_EVERY - 1
-                    scale_and_group(
-                        nc.gpsimd if on_gpsimd else nc.vector,
-                        grouped[v][:, i * n : (i + 1) * n],
-                        gu_raw[job][c][:, i, :, half * PAIRS : (half + 1) * PAIRS],
-                        gu_factors[job][:] if on_gpsimd else gu_spread[job][:],
-                    )
+                nc.vector.tensor_tensor(
+                    out=grouped[v][:].rearrange("p (g w j) -> p g w j", g=CHUNK, j=PACK),
+                    in0=gu_raw[job][c][:, :, :, half * PAIRS : (half + 1) * PAIRS].rearrange(
+                        "p g j w -> p g w j"
+                    ),
+                    in1=gu_spread[job][:]
+                    .unsqueeze(1)
+                    .unsqueeze(3)
+                    .to_broadcast([P, CHUNK, PAIRS, PACK]),
+                    op=ALU.mult,
+                )
             else:
                 b = v - GU_TILES
-                for unit in reversed(range(2)):
-                    on_gpsimd = (2 * b + unit) % GPSIMD_EVERY == GPSIMD_EVERY - 1
-                    spread_pair = down_spread[b][:, 2 * unit : 2 * unit + 2, :]
-                    scale_and_group(
-                        nc.gpsimd if on_gpsimd else nc.vector,
-                        grouped[v][:, unit * n : (unit + 1) * n],
-                        down_rows(b, unit),
-                        copy_for_gpsimd(spread_pair)[:] if on_gpsimd else spread_pair,
-                    )
+                first = (b % (D_LOAD // BANK)) * BANK
+                nc.vector.tensor_tensor(
+                    out=grouped[v][:, 0 : BANK * PACK].rearrange("p (w t) -> p w t", t=PACK),
+                    in0=down_raw[b // (D_LOAD // BANK)][:, :, first : first + BANK].rearrange(
+                        "p t w -> p w t"
+                    ),
+                    in1=down_spread[b][:].unsqueeze(2).to_broadcast([P, BANK, PACK]),
+                    op=ALU.mult,
+                )
 
         def quantise(v):
             words = CHUNK * PAIRS if v < GU_TILES else BANK
@@ -338,11 +323,11 @@ def tile_npertokenswishglu_k_kernel(tc, x, W_gate, W_up, W_down, s_u, s_v, out):
                 start=True,
                 stop=True,
             )
-            nc.scalar.copy(out=o_cols(b * BANK, BANK), in_=o_bank[:])
             squares = junk.tile([P, BANK], BF16, tag="squares")
             nc.scalar.activation(
                 out=squares[:], in_=o_bank[:], func=ACT.Square, accum_out=o_squares[:, b : b + 1]
             )
+            nc.scalar.copy(out=o_cols(b * BANK, BANK), in_=o_bank[:])
 
         for s in range(STEPS_AHEAD):
             squares_step(s)
@@ -355,7 +340,7 @@ def tile_npertokenswishglu_k_kernel(tc, x, W_gate, W_up, W_down, s_u, s_v, out):
                     load_down(c)
             if GU_TILES <= v + 1 < TILES:
                 b = v + 1 - GU_TILES
-                down_spread[b] = spread_over_partitions(down_inverse[:, b, :], 4)
+                down_spread[b] = spread_over_partitions(down_inverse[:, b, :], 2)
             if v < TILES:
                 scale(v)
             if 1 <= v <= TILES:

@@ -14,6 +14,7 @@ ALU = mybir.AluOpType
 AX = mybir.AxisListType
 
 P = 128
+NEAR = 4
 PACK = 4
 K_PASS = P * PACK
 TOKENS = 128
@@ -245,11 +246,16 @@ def tile_npertokenswishglu_k_kernel(tc, x, W_gate, W_up, W_down, s_u, s_v, out):
                 b = v - GU_TILES
                 first = (b % (D_LOAD // BANK)) * BANK
                 nc.vector.tensor_tensor(
-                    out=grouped[v][:, 0 : BANK * PACK].rearrange("p (w t) -> p w t", t=PACK),
-                    in0=down_raw[b // (D_LOAD // BANK)][:, :, first : first + BANK].rearrange(
-                        "p t w -> p w t"
+                    out=grouped[v][:, 0 : BANK * PACK].rearrange(
+                        "p (c i t) -> p c t i", i=NEAR, t=PACK
                     ),
-                    in1=down_spread[b][:].unsqueeze(2).to_broadcast([P, BANK, PACK]),
+                    in0=down_raw[b // (D_LOAD // BANK)][:, :, first : first + BANK].rearrange(
+                        "p t (c i) -> p c t i", i=NEAR
+                    ),
+                    in1=down_spread[b][:]
+                    .rearrange("p (c i) -> p c i", i=NEAR)
+                    .unsqueeze(2)
+                    .to_broadcast([P, BANK // NEAR, PACK, NEAR]),
                     op=ALU.mult,
                 )
 

@@ -11,7 +11,6 @@ U8 = mybir.dt.uint8
 FP8X4 = mybir.dt.float8_e4m3fn_x4
 ACT = mybir.ActivationFunctionType
 ALU = mybir.AluOpType
-AX = mybir.AxisListType
 
 P = 128
 NEAR = 4
@@ -20,20 +19,20 @@ K_PASS = P * PACK
 TOKENS = 128
 D_MODEL = 8192
 HIDDEN = 512
+GROUPS = HIDDEN // P
 PASSES = D_MODEL // K_PASS
 CHUNK = 4
-PAIRS = 2 * P
+CHUNKS = PASSES // CHUNK
 BANK = 512
-D_LOAD = 2048
-NORM_FLOOR = 1e-12
-GU_TILES = 4 * (PASSES // CHUNK)
 BLOCKS = D_MODEL // BANK
-TILES = GU_TILES + BLOCKS
-GU_STEPS = 4 * PASSES
-STEPS = GU_STEPS + 2 * BLOCKS
-STEPS_AHEAD = PASSES + 3
-STEPS_PER_TILE = 4
-SPREAD_LAG = 3
+D_LOAD = 2048
+D_PER_LOAD = D_LOAD // BANK
+NORM_FLOOR = 1e-12
+WORDS = 1024
+EARLY = 8
+GU_BANKS = 8
+STEPS_AHEAD = 4
+LAG = 2
 STORE = 1024
 
 FLOPS = 3 * 2 * TOKENS * D_MODEL * HIDDEN
@@ -46,12 +45,56 @@ def tile_npertokenswishglu_k_kernel(tc, x, W_gate, W_up, W_down, s_u, s_v, out):
         big = ctx.enter_context(tc.tile_pool(name="big", bufs=9))
         work = ctx.enter_context(tc.tile_pool(name="work", bufs=3))
         packed = ctx.enter_context(tc.tile_pool(name="packed", bufs=4))
-        junk = ctx.enter_context(tc.tile_pool(name="junk", bufs=4))
+        early = ctx.enter_context(tc.tile_pool(name="early", bufs=EARLY))
+        junk = ctx.enter_context(tc.tile_pool(name="junk", bufs=2))
         small = ctx.enter_context(tc.tile_pool(name="small", bufs=4))
         turned_pool = ctx.enter_context(tc.psum_pool(name="turned_pool", bufs=3))
         spread_pool = ctx.enter_context(tc.psum_pool(name="spread_pool", bufs=2))
         acc_pool = ctx.enter_context(tc.psum_pool(name="acc_pool", bufs=3))
         ctx.enter_context(tc.manual_schedule())
+
+        down_view = W_down.rearrange("l (t p) d -> p (l t) d", p=P)
+        down_raw = []
+
+        def load_down(pieces):
+            raw = big.tile([P, PACK, D_LOAD], BF16, tag="big", name="down_raw")
+            first = len(down_raw) * D_LOAD
+            width = D_LOAD // pieces
+            for i in range(pieces):
+                nc.sync.dma_start(
+                    out=raw[:, :, i * width : (i + 1) * width],
+                    in_=down_view[:, :, first + i * width : first + (i + 1) * width],
+                )
+            down_raw.append(raw)
+
+        x_view = x.rearrange("b l d -> b (l d)")
+
+        def load_x():
+            raw = big.tile([P, D_MODEL], BF16, tag="big", name="x_raw")
+            for c in range(CHUNKS):
+                cols = slice(c * CHUNK * K_PASS, (c + 1) * CHUNK * K_PASS)
+                nc.sync.dma_start(out=raw[:, cols], in_=x_view[:, cols])
+            return raw
+
+        gu_raw = [[], []]
+
+        def load_gate_or_up(which):
+            view = (W_gate, W_up)[which].rearrange("l (g p j) f -> p (l g) (j f)", p=P, j=PACK)
+            raw = big.tile([P, CHUNK, PACK, HIDDEN], BF16, tag="big", name="gu_raw")
+            for i in range(CHUNK):
+                nc.sync.dma_start(
+                    out=raw[:, i, :, :].rearrange("p j f -> p (j f)"),
+                    in_=view[:, len(gu_raw[which]) * CHUNK + i, :],
+                )
+            gu_raw[which].append(raw)
+
+        load_down(4)
+        x_raw = load_x()
+        load_down(1)
+        for c in range(CHUNKS):
+            load_gate_or_up(0)
+        for c in range(2):
+            load_gate_or_up(1)
 
         ident = const.tile([P, P], F32, tag="ident")
         make_identity(nc, ident[:])
@@ -64,35 +107,11 @@ def tile_npertokenswishglu_k_kernel(tc, x, W_gate, W_up, W_down, s_u, s_v, out):
         nc.scalar.dma_start(out=gain_rows[0:4, :], in_=s_u.rearrange("o (t c) -> (o t) c", c=P))
         nc.scalar.dma_start(out=gain_rows[4:8, :], in_=s_v.rearrange("o (t c) -> (o t) c", c=P))
 
-        x_view = x.rearrange("b l d -> b (l d)")
-        x_raw = big.tile([P, D_MODEL], BF16, tag="big")
-        for c in range(PASSES // CHUNK):
-            cols = slice(c * CHUNK * K_PASS, (c + 1) * CHUNK * K_PASS)
-            nc.sync.dma_start(out=x_raw[:, cols], in_=x_view[:, cols])
-
-        def load_gate_or_up(weight, c):
-            view = weight.rearrange("l (g p j) f -> p (l g) (j f)", p=P, j=PACK)
-            raw = big.tile([P, CHUNK, PACK, HIDDEN], BF16, tag="big")
-            for i in range(CHUNK):
-                nc.sync.dma_start(
-                    out=raw[:, i, :, :].rearrange("p j f -> p (j f)"), in_=view[:, c * CHUNK + i, :]
-                )
-            return raw
-
-        gate_raw = [load_gate_or_up(W_gate, c) for c in range(PASSES // CHUNK)]
-        up_raw = [load_gate_or_up(W_up, c) for c in range(PASSES // CHUNK)]
-        down_raw = []
-
-        def load_down(c):
-            view = W_down.rearrange("l (t p) d -> p (l t) d", p=P)
-            raw = big.tile([P, PACK, D_LOAD], BF16, tag="big")
-            nc.sync.dma_start(out=raw[:], in_=view[:, :, c * D_LOAD : (c + 1) * D_LOAD])
-            down_raw.append(raw)
-
         x_words = x_raw[:].bitcast(F32).rearrange("b (g p u) -> b g u p", p=P, u=2)
         x_codes = const.tile([P, PASSES, TOKENS], U32, tag="x_codes", align_bytes=64)
         x_plane = const.tile([P, PASSES, TOKENS], U8, tag="x_plane", align_bytes=64)
-        for c in range(PASSES // CHUNK):
+
+        def prepare_x(c):
             x_grouped = work.tile([P, CHUNK, TOKENS * PACK], BF16, tag="grouped", align_bytes=64)
             x_grouped_words = x_grouped[:].bitcast(F32)
             for h in range(2):
@@ -115,27 +134,25 @@ def tile_npertokenswishglu_k_kernel(tc, x, W_gate, W_up, W_down, s_u, s_v, out):
                 scales=x_plane[:, passes, :].rearrange("p g b -> p (g b)"),
                 in_=x_grouped[:].rearrange("p g n -> p (g n)"),
             )
-        load_down(0)
 
-        gain_cols = turned_pool.tile([P, P], BF16, tag="turned")
-        nc.tensor.transpose(gain_cols[:], gain_rows[:], ident_bf[:])
-        gains = const.tile([P, 8], F32, tag="gains")
-        nc.vector.tensor_copy(out=gains[:], in_=gain_cols[:, 0:8])
         sizes = const.tile([P, 8], F32, tag="sizes")
-        nc.vector.scalar_tensor_tensor(
-            out=sizes[:], in0=gains[:], scalar=-1.0, in1=gains[:], op0=ALU.mult, op1=ALU.max
-        )
-        nc.vector.tensor_scalar_mul(
-            out=sizes[:, 4:8], in0=sizes[:, 4:8], scalar1=math.sqrt(float(D_MODEL))
-        )
 
-        def add_up_squares(bank, sums):
-            halves = bank[:].bitcast(BF16).rearrange("q (k e) -> q k e", e=2)
-            for e in range(2):
-                squares = junk.tile([P, BANK], BF16, tag="squares")
-                nc.scalar.activation(
-                    out=squares[:], in_=halves[:, :, e], func=ACT.Square, accum_out=sums[e]
-                )
+        def prepare_gains():
+            gain_cols = turned_pool.tile([P, P], BF16, tag="turned")
+            nc.tensor.transpose(gain_cols[:], gain_rows[:], ident_bf[:])
+            gains = const.tile([P, 8], F32, tag="gains")
+            nc.vector.tensor_copy(out=gains[:], in_=gain_cols[:, 0:8])
+            nc.vector.scalar_tensor_tensor(
+                out=sizes[:], in0=gains[:], scalar=-1.0, in1=gains[:], op0=ALU.mult, op1=ALU.max
+            )
+            nc.vector.tensor_scalar_mul(
+                out=sizes[:, 4:8], in0=sizes[:, 4:8], scalar1=math.sqrt(float(D_MODEL))
+            )
+
+        gu_inverse = const.tile([P, 2, GROUPS], F32, tag="gu_inverse")
+        down_inverse = const.tile([P, BLOCKS, 4], F32, tag="down_inverse")
+        gu_sums = {}
+        down_sums = {}
 
         def one_over_norm(inverse, sum_of_squares, width):
             floored = small.tile([P, width], F32, tag="floored")
@@ -146,74 +163,145 @@ def tile_npertokenswishglu_k_kernel(tc, x, W_gate, W_up, W_down, s_u, s_v, out):
                 out=inverse, in0=floored[:], in1=minus_half[:, 0:width], op=ALU.pow
             )
 
-        def spread_over_partitions(inverse, groups):
-            spread = spread_pool.tile([P, groups * PAIRS], F32, tag="spread")
-            by_half = spread[:].rearrange("p (n q e) -> p n e q", q=P, e=2)
-            for n in range(groups):
-                for e in range(2):
-                    c = 2 * n + e
-                    nc.tensor.transpose(
-                        by_half[:, n, e, :], inverse[:, c : c + 1].to_broadcast([P, P]), ident[:]
-                    )
+        def add_up_squares(turned, accum):
+            squares = junk.tile([P, 2 * BANK], BF16, tag="squares")
+            nc.scalar.activation(
+                out=squares[:, 0 : turned.shape[1]], in_=turned, func=ACT.Square, accum_out=accum
+            )
+
+        def gu_columns(which, group, g, j):
+            return gu_raw[which][g // CHUNK][:, g % CHUNK, j, group * P : (group + 1) * P]
+
+        def gu_step(which, group, i):
+            if i == 0:
+                gu_sums[which, group] = small.tile([P, GU_BANKS], F32, tag="gu_sums", name="gu_sums")
+            bank = turned_pool.tile([P, 2 * BANK], BF16, tag="turned")
+            for n in range(2 * PACK):
+                nc.tensor.transpose(
+                    bank[:, n * P : (n + 1) * P],
+                    gu_columns(which, group, 2 * i + n // PACK, n % PACK),
+                    ident_bf[:],
+                )
+            add_up_squares(bank[:], gu_sums[which, group][:, i : i + 1])
+            if i == GU_BANKS - 1:
+                copied = small.tile([P, GU_BANKS], F32, tag="copied")
+                total = small.tile([P, 1], F32, tag="total")
+                nc.scalar.activation(
+                    out=copied[:], in_=gu_sums[which, group][:], func=ACT.Copy, accum_out=total[:]
+                )
+                one_over_norm(gu_inverse[:, which, group : group + 1], total[:], 1)
+
+        def down_step(b, i):
+            if i == 0:
+                down_sums[b] = small.tile([P, 4], F32, tag="down_sums", name="down_sums")
+            raw = down_raw[b // D_PER_LOAD]
+            bank = turned_pool.tile([P, 2 * BANK], BF16, tag="turned")
+            for n in range(2 * PACK):
+                first = (b % D_PER_LOAD) * BANK + (2 * i + n // PACK) * P
+                nc.tensor.transpose(
+                    bank[:, n * P : (n + 1) * P], raw[:, n % PACK, first : first + P], ident_bf[:]
+                )
+            for e in range(2):
+                add_up_squares(
+                    bank[:, e * BANK : (e + 1) * BANK],
+                    down_sums[b][:, 2 * i + e : 2 * i + e + 1],
+                )
+            if i == 1:
+                one_over_norm(down_inverse[:, b, :], down_sums[b][:], 4)
+
+        gram = []
+
+        def gram_pass(g):
+            if g == 0:
+                gram.append(acc_pool.tile([P, P], F32, tag="acc", name="gram"))
+            for j in range(PACK):
+                columns = gu_columns(0, 0, g, j)
+                nc.tensor.matmul(
+                    gram[0][:],
+                    lhsT=columns,
+                    rhs=columns,
+                    start=(g == 0 and j == 0),
+                    stop=(g == PASSES - 1 and j == PACK - 1),
+                )
+            if g == PASSES - 1:
+                diagonal = const.tile([P, P], F32, tag="diagonal")
+                total = small.tile([P, 1], F32, tag="total")
+                nc.vector.scalar_tensor_tensor(
+                    out=diagonal[:],
+                    in0=gram[0][:],
+                    scalar=1.0,
+                    in1=ident[:],
+                    op0=ALU.mult,
+                    op1=ALU.mult,
+                    accum_out=total[:],
+                )
+                one_over_norm(gu_inverse[:, 0, 0:1], total[:], 1)
+
+        steps = []
+        ready = {}
+
+        def list_down(b):
+            for i in range(2):
+                steps.append((down_step, b, i))
+            ready["down", b] = len(steps)
+
+        for b in range(EARLY):
+            list_down(b)
+        first_gu_step = len(steps)
+        ready[0, 0] = first_gu_step + GU_BANKS
+        for which in range(2):
+            for group in range(GROUPS):
+                if (which, group) != (0, 0):
+                    for i in range(GU_BANKS):
+                        steps.append((gu_step, which, group, i))
+                    ready[which, group] = len(steps)
+        for b in range(EARLY, BLOCKS):
+            list_down(b)
+        emitted = [0]
+
+        def emit_steps(upto):
+            for s in range(emitted[0], min(upto, len(steps))):
+                if first_gu_step <= s < first_gu_step + GU_BANKS:
+                    for g in range(2):
+                        gram_pass(2 * (s - first_gu_step) + g)
+                steps[s][0](*steps[s][1:])
+                emitted[0] = s + 1
+
+        tiles = [("down", b) for b in range(EARLY)]
+        for which, group, count in ((0, 0, 1), (0, 1, 1), (0, 2, 2), (1, 0, 2), (1, 2, 2)):
+            passes = WORDS // (count * P)
+            for g in range(0, PASSES, passes):
+                tiles.append((which, group, count, g, passes))
+        last_gu = len(tiles) - 1
+        tiles = tiles + [("down", b) for b in range(EARLY, BLOCKS)]
+
+        def unit_of(tile_):
+            return tile_ if tile_[0] == "down" else tile_[0:3]
+
+        def spread_over_partitions(unit):
+            spread = spread_pool.tile([P, BANK], F32, tag="spread", name="spread")
+            if unit[0] == "down":
+                factors = [down_inverse[:, unit[1], n : n + 1] for n in range(4)]
+            else:
+                which, group, count = unit
+                factors = [gu_inverse[:, which, group + n : group + n + 1] for n in range(count)]
+            for n in range(len(factors)):
+                nc.tensor.transpose(
+                    spread[:, n * P : (n + 1) * P], factors[n].to_broadcast([P, P]), ident[:]
+                )
             return spread
 
-        gu_raw = [gate_raw, gate_raw, up_raw, up_raw]
-        gu_sums = [None] * 4
-        gu_inverse = const.tile([P, 4, 2], F32, tag="gu_inverse")
-        gu_spread = [None] * 4
-        down_inverse = const.tile([P, BLOCKS, 4], F32, tag="down_inverse")
-        down_sums = [None] * BLOCKS
-        down_spread = [None] * BLOCKS
+        def last_step(unit):
+            if unit[0] == "down":
+                return ready[unit]
+            return max(ready[unit[0], unit[1] + n] for n in range(unit[2]))
 
-        def down_rows(b, unit):
-            first = (b % (D_LOAD // BANK)) * BANK + unit * PAIRS
-            return down_raw[b // (D_LOAD // BANK)][:, :, first : first + PAIRS]
-
-        def squares_step(s):
-            bank = turned_pool.tile([P, BANK], F32, tag="turned")
-            if s < GU_STEPS:
-                job, g = s // PASSES, s % PASSES
-                half = job % 2
-                if g == 0:
-                    gu_sums[job] = small.tile([P, 2, PASSES], F32, tag="gu_sums", name="gu_sums")
-                words = gu_raw[job][g // CHUNK][:, g % CHUNK, :, :].bitcast(F32)
-                for j in range(PACK):
-                    nc.tensor.transpose(
-                        bank[:, j * P : (j + 1) * P], words[:, j, half * P : (half + 1) * P], ident[:]
-                    )
-                add_up_squares(bank, [gu_sums[job][:, e, g : g + 1] for e in range(2)])
-                if g == PASSES - 1:
-                    total = small.tile([P, 2], F32, tag="total")
-                    for e in range(2):
-                        copied = small.tile([P, PASSES], F32, tag="copied")
-                        nc.scalar.activation(
-                            out=copied[:],
-                            in_=gu_sums[job][:, e, :],
-                            func=ACT.Copy,
-                            accum_out=total[:, e : e + 1],
-                        )
-                    one_over_norm(gu_inverse[:, job, :], total[:], 2)
-            else:
-                b, unit = (s - GU_STEPS) // 2, (s - GU_STEPS) % 2
-                if unit == 0:
-                    down_sums[b] = small.tile([P, 4], F32, tag="down_sums", name="down_sums")
-                words = down_rows(b, unit).bitcast(F32)
-                for t in range(PACK):
-                    nc.tensor.transpose(bank[:, t * P : (t + 1) * P], words[:, t, :], ident[:])
-                add_up_squares(
-                    bank, [down_sums[b][:, 2 * unit + e : 2 * unit + e + 1] for e in range(2)]
-                )
-                if unit == 1:
-                    one_over_norm(down_inverse[:, b, :], down_sums[b][:], 4)
-            if s >= PASSES + SPREAD_LAG - 1 and (s - SPREAD_LAG + 1) % PASSES == 0 and s < GU_STEPS + PASSES:
-                job = (s - SPREAD_LAG + 1) // PASSES - 1
-                gu_spread[job] = spread_over_partitions(gu_inverse[:, job, :], 1)
-
-        grouped = [None] * TILES
-        codes = [None] * TILES
-        plane = [None] * TILES
-        acc = [None] * 4
-        u_scaled = const.tile([P, PACK, TOKENS], F32, tag="u_scaled")
+        spreads = {}
+        grouped = {}
+        codes = {}
+        plane = {}
+        acc = {}
+        u_scaled = const.tile([P, GROUPS, TOKENS], F32, tag="u_scaled")
         h_grouped = const.tile([P, TOKENS, PACK], BF16, tag="h_grouped", align_bytes=64)
         h_codes = const.tile([P, TOKENS], U32, tag="h_codes", align_bytes=64)
         h_plane = const.tile([P, TOKENS], U8, tag="h_plane", align_bytes=64)
@@ -225,44 +313,53 @@ def tile_npertokenswishglu_k_kernel(tc, x, W_gate, W_up, W_down, s_u, s_v, out):
             return o_sb[first // half][:, first % half : first % half + width]
 
         def scale(v):
-            grouped[v] = work.tile(
-                [P, CHUNK * PAIRS * PACK], BF16, tag="grouped", align_bytes=64, name="grouped"
-            )
-            if v < GU_TILES:
-                job, c = v // (PASSES // CHUNK), v % (PASSES // CHUNK)
-                half = job % 2
-                nc.vector.tensor_tensor(
-                    out=grouped[v][:].rearrange("p (g w j) -> p g w j", g=CHUNK, j=PACK),
-                    in0=gu_raw[job][c][:, :, :, half * PAIRS : (half + 1) * PAIRS].rearrange(
-                        "p g j w -> p g w j"
-                    ),
-                    in1=gu_spread[job][:]
-                    .unsqueeze(1)
-                    .unsqueeze(3)
-                    .to_broadcast([P, CHUNK, PAIRS, PACK]),
-                    op=ALU.mult,
-                )
-            else:
-                b = v - GU_TILES
-                first = (b % (D_LOAD // BANK)) * BANK
+            grouped[v] = work.tile([P, WORDS * PACK], BF16, tag="grouped", align_bytes=64, name="grouped")
+            spread = spreads[unit_of(tiles[v])]
+            if tiles[v][0] == "down":
+                b = tiles[v][1]
+                first = (b % D_PER_LOAD) * BANK
                 nc.vector.tensor_tensor(
                     out=grouped[v][:, 0 : BANK * PACK].rearrange(
                         "p (c i t) -> p c t i", i=NEAR, t=PACK
                     ),
-                    in0=down_raw[b // (D_LOAD // BANK)][:, :, first : first + BANK].rearrange(
+                    in0=down_raw[b // D_PER_LOAD][:, :, first : first + BANK].rearrange(
                         "p t (c i) -> p c t i", i=NEAR
                     ),
-                    in1=down_spread[b][:]
+                    in1=spread[:]
                     .rearrange("p (c i) -> p c i", i=NEAR)
                     .unsqueeze(2)
                     .to_broadcast([P, BANK // NEAR, PACK, NEAR]),
                     op=ALU.mult,
                 )
+                return
+            which, group, count, g0, passes = tiles[v]
+            width = count * P
+            size = width * PACK
+            for n in range(passes):
+                g = g0 + n
+                nc.vector.tensor_tensor(
+                    out=grouped[v][:, n * size : (n + 1) * size].rearrange(
+                        "p (c i j) -> p c j i", i=NEAR, j=PACK
+                    ),
+                    in0=gu_raw[which][g // CHUNK][
+                        :, g % CHUNK, :, group * P : group * P + width
+                    ].rearrange("p j (c i) -> p c j i", i=NEAR),
+                    in1=spread[:, 0:width]
+                    .rearrange("p (c i) -> p c i", i=NEAR)
+                    .unsqueeze(2)
+                    .to_broadcast([P, width // NEAR, PACK, NEAR]),
+                    op=ALU.mult,
+                )
 
         def quantise(v):
-            words = CHUNK * PAIRS if v < GU_TILES else BANK
-            codes[v] = packed.tile([P, CHUNK * PAIRS], U32, tag="codes", align_bytes=64, name="codes")
-            plane[v] = packed.tile([P, CHUNK * PAIRS], U8, tag="plane", align_bytes=64, name="plane")
+            is_early = v < EARLY
+            words = BANK if tiles[v][0] == "down" else WORDS
+            if is_early:
+                codes[v] = early.tile([P, BANK], U32, tag="early_codes", align_bytes=64, name="early_codes")
+                plane[v] = early.tile([P, BANK], U8, tag="early_plane", align_bytes=64, name="early_plane")
+            else:
+                codes[v] = packed.tile([P, WORDS], U32, tag="codes", align_bytes=64, name="codes")
+                plane[v] = packed.tile([P, WORDS], U8, tag="plane", align_bytes=64, name="plane")
             nc.vector.quantize_mx(
                 out=codes[v][:, 0:words].bitcast(FP8X4),
                 scales=plane[v][:, 0:words],
@@ -270,17 +367,17 @@ def tile_npertokenswishglu_k_kernel(tc, x, W_gate, W_up, W_down, s_u, s_v, out):
             )
 
         def multiply_gate_up(v):
-            job, c = v // (PASSES // CHUNK), v % (PASSES // CHUNK)
-            if c == 0:
-                acc[job] = [
-                    acc_pool.tile([P, TOKENS], F32, tag="acc", name="acc%d" % m) for m in range(2)
-                ]
-            for m in range(2):
-                for i in range(CHUNK):
-                    g = c * CHUNK + i
-                    cols = slice(i * PAIRS + m * P, i * PAIRS + (m + 1) * P)
+            which, group, count, g0, passes = tiles[v]
+            width = count * P
+            for m in range(count):
+                t = group + m
+                if g0 == 0:
+                    acc[which, t] = acc_pool.tile([P, TOKENS], F32, tag="acc", name="acc")
+                for i in range(passes):
+                    g = g0 + i
+                    cols = slice(i * width + m * P, i * width + (m + 1) * P)
                     nc.tensor.matmul_mx(
-                        out=acc[job][m][:],
+                        out=acc[which, t][:],
                         lhsT=codes[v][:, cols].bitcast(FP8X4),
                         lhsT_scale=plane[v][:, cols],
                         rhs=x_codes[:, g, :].bitcast(FP8X4),
@@ -288,26 +385,26 @@ def tile_npertokenswishglu_k_kernel(tc, x, W_gate, W_up, W_down, s_u, s_v, out):
                         start=(g == 0),
                         stop=(g == PASSES - 1),
                     )
-            if c < PASSES // CHUNK - 1:
+            if g0 + passes < PASSES:
                 return
-            for m in range(2):
-                t = 2 * (job % 2) + m
-                if job < 2:
+            for m in range(count):
+                t = group + m
+                if which == 0:
                     nc.scalar.activation(
                         out=u_scaled[:, t, :],
-                        in_=acc[job][m][:],
+                        in_=acc[which, t][:],
                         func=ACT.Copy,
                         scale=sizes[:, t : t + 1],
                     )
                 else:
                     swish = small.tile([P, TOKENS], F32, tag="swish")
                     nc.scalar.activation(
-                        out=swish[:], in_=acc[job][m][:], func=ACT.Silu, scale=sizes[:, 4 + t : 5 + t]
+                        out=swish[:], in_=acc[which, t][:], func=ACT.Silu, scale=sizes[:, 4 + t : 5 + t]
                     )
                     nc.vector.tensor_tensor(
                         out=h_grouped[:, :, t], in0=swish[:], in1=u_scaled[:, t, :], op=ALU.mult
                     )
-            if job == 3:
+            if v == last_gu:
                 nc.vector.quantize_mx(
                     out=h_codes[:].bitcast(FP8X4),
                     scales=h_plane[:],
@@ -315,11 +412,11 @@ def tile_npertokenswishglu_k_kernel(tc, x, W_gate, W_up, W_down, s_u, s_v, out):
                 )
 
         def multiply_down(v):
-            b = v - GU_TILES
-            if b == 0:
+            b = tiles[v][1]
+            if not o_sb:
                 for i in range(2):
-                    o_sb.append(big.tile([P, D_MODEL // 2], F32, tag="big", name="o_sb%d" % i))
-            o_bank = acc_pool.tile([P, BANK], F32, tag="acc")
+                    o_sb.append(big.tile([P, D_MODEL // 2], F32, tag="big", name="o_sb"))
+            o_bank = acc_pool.tile([P, BANK], F32, tag="acc", name="o_bank")
             nc.tensor.matmul_mx(
                 out=o_bank[:],
                 lhsT=h_codes[:].bitcast(FP8X4),
@@ -329,36 +426,51 @@ def tile_npertokenswishglu_k_kernel(tc, x, W_gate, W_up, W_down, s_u, s_v, out):
                 start=True,
                 stop=True,
             )
-            squares = junk.tile([P, BANK], BF16, tag="squares")
+            squares = junk.tile([P, 2 * BANK], BF16, tag="squares")
             nc.scalar.activation(
-                out=squares[:], in_=o_bank[:], func=ACT.Square, accum_out=o_squares[:, b : b + 1]
+                out=squares[:, 0:BANK], in_=o_bank[:], func=ACT.Square, accum_out=o_squares[:, b : b + 1]
             )
             nc.scalar.copy(out=o_cols(b * BANK, BANK), in_=o_bank[:])
 
-        for s in range(STEPS_AHEAD):
-            squares_step(s)
-        for v in range(TILES + 2):
-            first = STEPS_AHEAD + v * STEPS_PER_TILE
-            for s in range(min(first, STEPS), min(first + STEPS_PER_TILE, STEPS)):
-                squares_step(s)
-            if v == 2 * (PASSES // CHUNK):
-                for c in range(1, D_MODEL // D_LOAD):
-                    load_down(c)
-            if GU_TILES <= v + 1 < TILES:
-                b = v + 1 - GU_TILES
-                down_spread[b] = spread_over_partitions(down_inverse[:, b, :], 2)
-            if v < TILES:
+        emit_steps(ready["down", 0] + LAG)
+        spreads[unit_of(tiles[0])] = spread_over_partitions(unit_of(tiles[0]))
+        target = STEPS_AHEAD
+        waiting = []
+        multiplied = 0
+        for v in range(len(tiles) + 2):
+            if v < len(tiles):
                 scale(v)
-            if 1 <= v <= TILES:
+            if 1 <= v <= len(tiles):
                 quantise(v - 1)
-            if 2 <= v and v - 2 < GU_TILES:
-                multiply_gate_up(v - 2)
-            if v - 2 >= GU_TILES:
-                multiply_down(v - 2)
+            if v == 0:
+                prepare_gains()
+            if 1 <= v < 1 + CHUNKS:
+                prepare_x(v - 1)
+            if v == D_PER_LOAD or v == 2 * D_PER_LOAD:
+                load_gate_or_up(1)
+            if v == 2 * D_PER_LOAD:
+                load_down(1)
+            if v == EARLY + 8:
+                load_down(1)
+            if v + 1 < len(tiles) and unit_of(tiles[v + 1]) not in spreads:
+                unit = unit_of(tiles[v + 1])
+                emit_steps(last_step(unit) + LAG)
+                spreads[unit] = spread_over_partitions(unit)
+            target = target + (3 if v < EARLY else 4)
+            emit_steps(target)
+            if v >= 2:
+                if tiles[v - 2][0] == "down":
+                    waiting.append(v - 2)
+                else:
+                    multiply_gate_up(v - 2)
+            if v - 2 > last_gu:
+                for w in waiting[multiplied : multiplied + 3]:
+                    multiply_down(w)
+                    multiplied = multiplied + 1
 
         o_total = small.tile([P, 1], F32, tag="o_total")
-        copied = small.tile([P, BLOCKS], F32, tag="copied")
-        nc.scalar.activation(out=copied[:], in_=o_squares[:], func=ACT.Copy, accum_out=o_total[:])
+        o_copied = small.tile([P, BLOCKS], F32, tag="o_copied")
+        nc.scalar.activation(out=o_copied[:], in_=o_squares[:], func=ACT.Copy, accum_out=o_total[:])
         o_inverse = small.tile([P, 1], F32, tag="o_inverse")
         one_over_norm(o_inverse[:], o_total[:], 1)
         out_view = out.rearrange("b l d -> b (l d)")

@@ -34,6 +34,7 @@ GU_BANKS = 8
 STEPS_AHEAD = 4
 LAG = 2
 STORE = 1024
+IN_PSUM = 2
 
 FLOPS = 3 * 2 * TOKENS * D_MODEL * HIDDEN
 
@@ -56,25 +57,21 @@ def tile_npertokenswishglu_k_kernel(tc, x, W_gate, W_up, W_down, s_u, s_v, out):
         down_view = W_down.rearrange("l (t p) d -> p (l t) d", p=P)
         down_raw = []
 
-        def load_down(pieces):
-            raw = big.tile([P, PACK, D_LOAD], BF16, tag="big", name="down_raw")
-            first = len(down_raw) * D_LOAD
-            width = D_LOAD // pieces
-            for i in range(pieces):
-                nc.sync.dma_start(
-                    out=raw[:, :, i * width : (i + 1) * width],
-                    in_=down_view[:, :, first + i * width : first + (i + 1) * width],
-                )
-            down_raw.append(raw)
+        def load_down_columns(first, width):
+            nc.sync.dma_start(
+                out=down_raw[first // D_LOAD][:, :, first % D_LOAD : first % D_LOAD + width],
+                in_=down_view[:, :, first : first + width],
+            )
+
+        def load_down():
+            down_raw.append(big.tile([P, PACK, D_LOAD], BF16, tag="big", name="down_raw"))
+            load_down_columns((len(down_raw) - 1) * D_LOAD, D_LOAD)
 
         x_view = x.rearrange("b l d -> b (l d)")
 
-        def load_x():
-            raw = big.tile([P, D_MODEL], BF16, tag="big", name="x_raw")
-            for c in range(CHUNKS):
-                cols = slice(c * CHUNK * K_PASS, (c + 1) * CHUNK * K_PASS)
-                nc.sync.dma_start(out=raw[:, cols], in_=x_view[:, cols])
-            return raw
+        def load_x(c):
+            cols = slice(c * CHUNK * K_PASS, (c + 1) * CHUNK * K_PASS)
+            nc.sync.dma_start(out=x_raw[:, cols], in_=x_view[:, cols])
 
         gu_raw = [[], []]
 
@@ -88,9 +85,15 @@ def tile_npertokenswishglu_k_kernel(tc, x, W_gate, W_up, W_down, s_u, s_v, out):
                 )
             gu_raw[which].append(raw)
 
-        load_down(4)
-        x_raw = load_x()
-        load_down(1)
+        down_raw.append(big.tile([P, PACK, D_LOAD], BF16, tag="big", name="down_raw"))
+        x_raw = big.tile([P, D_MODEL], BF16, tag="big", name="x_raw")
+        load_down_columns(0, BANK)
+        load_x(0)
+        load_down_columns(BANK, BANK)
+        for c in range(1, CHUNKS):
+            load_x(c)
+        load_down_columns(2 * BANK, 2 * BANK)
+        load_down()
         for c in range(CHUNKS):
             load_gate_or_up(0)
         for c in range(2):
@@ -163,49 +166,71 @@ def tile_npertokenswishglu_k_kernel(tc, x, W_gate, W_up, W_down, s_u, s_v, out):
                 out=inverse, in0=floored[:], in1=minus_half[:, 0:width], op=ALU.pow
             )
 
-        def add_up_squares(turned, accum):
+        def add_up_squares(turned, width, accum):
             squares = junk.tile([P, 2 * BANK], BF16, tag="squares")
             nc.scalar.activation(
-                out=squares[:, 0 : turned.shape[1]], in_=turned, func=ACT.Square, accum_out=accum
+                out=squares[:, 0:width], in_=turned, func=ACT.Square, accum_out=accum
             )
 
-        def gu_columns(which, group, g, j):
-            return gu_raw[which][g // CHUNK][:, g % CHUNK, j, group * P : (group + 1) * P]
+        def turn_pairs(blocks, accums):
+            bank = turned_pool.tile([P, BANK], F32, tag="turned")
+            for n in range(PACK):
+                nc.tensor.transpose(bank[:, n * P : (n + 1) * P], blocks[n].bitcast(F32), ident[:])
+            halves = bank[:].bitcast(BF16).rearrange("q (k e) -> q k e", e=2)
+            for e in range(2):
+                add_up_squares(halves[:, :, e], BANK, accums[e])
 
-        def gu_step(which, group, i):
+        def gu_columns(which, group, count, g, j):
+            return gu_raw[which][g // CHUNK][:, g % CHUNK, j, group * P : (group + count) * P]
+
+        def close_gu(which, group, parts):
+            total = small.tile([P, 2], F32, tag="total")
+            for e in range(len(parts)):
+                copied = small.tile([P, PASSES], F32, tag="copied")
+                nc.scalar.activation(
+                    out=copied[:, 0 : parts[e].shape[1]],
+                    in_=parts[e],
+                    func=ACT.Copy,
+                    accum_out=total[:, e : e + 1],
+                )
+            width = len(parts)
+            one_over_norm(gu_inverse[:, which, group : group + width], total[:, 0:width], width)
+
+        def single_step(which, group, i):
             if i == 0:
-                gu_sums[which, group] = small.tile([P, GU_BANKS], F32, tag="gu_sums", name="gu_sums")
+                gu_sums[which, group] = small.tile([P, 2, PASSES], F32, tag="gu_sums", name="gu_sums")
             bank = turned_pool.tile([P, 2 * BANK], BF16, tag="turned")
             for n in range(2 * PACK):
                 nc.tensor.transpose(
                     bank[:, n * P : (n + 1) * P],
-                    gu_columns(which, group, 2 * i + n // PACK, n % PACK),
+                    gu_columns(which, group, 1, 2 * i + n // PACK, n % PACK),
                     ident_bf[:],
                 )
-            add_up_squares(bank[:], gu_sums[which, group][:, i : i + 1])
+            sums = gu_sums[which, group][:, 0, :]
+            add_up_squares(bank[:], 2 * BANK, sums[:, i : i + 1])
             if i == GU_BANKS - 1:
-                copied = small.tile([P, GU_BANKS], F32, tag="copied")
-                total = small.tile([P, 1], F32, tag="total")
-                nc.scalar.activation(
-                    out=copied[:], in_=gu_sums[which, group][:], func=ACT.Copy, accum_out=total[:]
-                )
-                one_over_norm(gu_inverse[:, which, group : group + 1], total[:], 1)
+                close_gu(which, group, [sums[:, 0:GU_BANKS]])
+
+        def pair_step(which, group, g):
+            if g == 0:
+                gu_sums[which, group] = small.tile([P, 2, PASSES], F32, tag="gu_sums", name="gu_sums")
+            sums = gu_sums[which, group]
+            turn_pairs(
+                [gu_columns(which, group, 2, g, j) for j in range(PACK)],
+                [sums[:, e, g : g + 1] for e in range(2)],
+            )
+            if g == PASSES - 1:
+                close_gu(which, group, [sums[:, e, :] for e in range(2)])
 
         def down_step(b, i):
             if i == 0:
                 down_sums[b] = small.tile([P, 4], F32, tag="down_sums", name="down_sums")
             raw = down_raw[b // D_PER_LOAD]
-            bank = turned_pool.tile([P, 2 * BANK], BF16, tag="turned")
-            for n in range(2 * PACK):
-                first = (b % D_PER_LOAD) * BANK + (2 * i + n // PACK) * P
-                nc.tensor.transpose(
-                    bank[:, n * P : (n + 1) * P], raw[:, n % PACK, first : first + P], ident_bf[:]
-                )
-            for e in range(2):
-                add_up_squares(
-                    bank[:, e * BANK : (e + 1) * BANK],
-                    down_sums[b][:, 2 * i + e : 2 * i + e + 1],
-                )
+            first = (b % D_PER_LOAD) * BANK + i * 2 * P
+            turn_pairs(
+                [raw[:, t, first : first + 2 * P] for t in range(PACK)],
+                [down_sums[b][:, 2 * i + e : 2 * i + e + 1] for e in range(2)],
+            )
             if i == 1:
                 one_over_norm(down_inverse[:, b, :], down_sums[b][:], 4)
 
@@ -215,7 +240,7 @@ def tile_npertokenswishglu_k_kernel(tc, x, W_gate, W_up, W_down, s_u, s_v, out):
             if g == 0:
                 gram.append(acc_pool.tile([P, P], F32, tag="acc", name="gram"))
             for j in range(PACK):
-                columns = gu_columns(0, 0, g, j)
+                columns = gu_columns(0, 0, 1, g, j)
                 nc.tensor.matmul(
                     gram[0][:],
                     lhsT=columns,
@@ -248,13 +273,14 @@ def tile_npertokenswishglu_k_kernel(tc, x, W_gate, W_up, W_down, s_u, s_v, out):
         for b in range(EARLY):
             list_down(b)
         first_gu_step = len(steps)
-        ready[0, 0] = first_gu_step + GU_BANKS
-        for which in range(2):
-            for group in range(GROUPS):
-                if (which, group) != (0, 0):
-                    for i in range(GU_BANKS):
-                        steps.append((gu_step, which, group, i))
-                    ready[which, group] = len(steps)
+        for i in range(GU_BANKS):
+            steps.append((single_step, 0, 1, i))
+        ready[0, 0, 1] = len(steps)
+        ready[0, 1, 1] = len(steps)
+        for which, group in ((0, 2), (1, 0), (1, 2)):
+            for g in range(PASSES):
+                steps.append((pair_step, which, group, g))
+            ready[which, group, 2] = len(steps)
         for b in range(EARLY, BLOCKS):
             list_down(b)
         emitted = [0]
@@ -280,21 +306,20 @@ def tile_npertokenswishglu_k_kernel(tc, x, W_gate, W_up, W_down, s_u, s_v, out):
 
         def spread_over_partitions(unit):
             spread = spread_pool.tile([P, BANK], F32, tag="spread", name="spread")
+            if unit[0] != "down" and unit[2] == 1:
+                factor = gu_inverse[:, unit[0], unit[1] : unit[1] + 1]
+                nc.tensor.transpose(spread[:, 0:P], factor.to_broadcast([P, P]), ident[:])
+                return spread
             if unit[0] == "down":
-                factors = [down_inverse[:, unit[1], n : n + 1] for n in range(4)]
+                factors = down_inverse[:, unit[1], :]
             else:
-                which, group, count = unit
-                factors = [gu_inverse[:, which, group + n : group + n + 1] for n in range(count)]
-            for n in range(len(factors)):
+                factors = gu_inverse[:, unit[0], unit[1] : unit[1] + 2]
+            by_half = spread[:].rearrange("p (n q e) -> p n e q", q=P, e=2)
+            for c in range(factors.shape[1]):
                 nc.tensor.transpose(
-                    spread[:, n * P : (n + 1) * P], factors[n].to_broadcast([P, P]), ident[:]
+                    by_half[:, c // 2, c % 2, :], factors[:, c : c + 1].to_broadcast([P, P]), ident[:]
                 )
             return spread
-
-        def last_step(unit):
-            if unit[0] == "down":
-                return ready[unit]
-            return max(ready[unit[0], unit[1] + n] for n in range(unit[2]))
 
         spreads = {}
         grouped = {}
@@ -306,6 +331,7 @@ def tile_npertokenswishglu_k_kernel(tc, x, W_gate, W_up, W_down, s_u, s_v, out):
         h_codes = const.tile([P, TOKENS], U32, tag="h_codes", align_bytes=64)
         h_plane = const.tile([P, TOKENS], U8, tag="h_plane", align_bytes=64)
         o_sb = []
+        o_banks = []
         o_squares = const.tile([P, BLOCKS], F32, tag="o_squares")
 
         def o_cols(first, width):
@@ -430,9 +456,18 @@ def tile_npertokenswishglu_k_kernel(tc, x, W_gate, W_up, W_down, s_u, s_v, out):
             nc.scalar.activation(
                 out=squares[:, 0:BANK], in_=o_bank[:], func=ACT.Square, accum_out=o_squares[:, b : b + 1]
             )
-            nc.scalar.copy(out=o_cols(b * BANK, BANK), in_=o_bank[:])
+            if b < BLOCKS - IN_PSUM:
+                nc.scalar.copy(out=o_cols(b * BANK, BANK), in_=o_bank[:])
+            else:
+                o_banks.append(o_bank)
 
+        emit_steps(1)
+        prepare_x(0)
+        emit_steps(ready["down", 0])
+        prepare_x(1)
         emit_steps(ready["down", 0] + LAG)
+        prepare_x(2)
+        prepare_x(3)
         spreads[unit_of(tiles[0])] = spread_over_partitions(unit_of(tiles[0]))
         target = STEPS_AHEAD
         waiting = []
@@ -444,17 +479,15 @@ def tile_npertokenswishglu_k_kernel(tc, x, W_gate, W_up, W_down, s_u, s_v, out):
                 quantise(v - 1)
             if v == 0:
                 prepare_gains()
-            if 1 <= v < 1 + CHUNKS:
-                prepare_x(v - 1)
             if v == D_PER_LOAD or v == 2 * D_PER_LOAD:
                 load_gate_or_up(1)
             if v == 2 * D_PER_LOAD:
-                load_down(1)
+                load_down()
             if v == EARLY + 8:
-                load_down(1)
+                load_down()
             if v + 1 < len(tiles) and unit_of(tiles[v + 1]) not in spreads:
                 unit = unit_of(tiles[v + 1])
-                emit_steps(last_step(unit) + LAG)
+                emit_steps(ready[unit] + LAG)
                 spreads[unit] = spread_over_partitions(unit)
             target = target + (3 if v < EARLY else 4)
             emit_steps(target)
@@ -474,7 +507,16 @@ def tile_npertokenswishglu_k_kernel(tc, x, W_gate, W_up, W_down, s_u, s_v, out):
         o_inverse = small.tile([P, 1], F32, tag="o_inverse")
         one_over_norm(o_inverse[:], o_total[:], 1)
         out_view = out.rearrange("b l d -> b (l d)")
-        for s in range(D_MODEL // STORE):
-            cols = o_cols(s * STORE, STORE)
-            nc.vector.tensor_scalar_mul(out=cols, in0=cols, scalar1=o_inverse[:, 0:1])
-            nc.sync.dma_start(out=out_view[:, s * STORE : (s + 1) * STORE], in_=cols)
+
+        def store(first, width, source):
+            cols = o_cols(first, width)
+            nc.vector.tensor_scalar_mul(out=cols, in0=source, scalar1=o_inverse[:, 0:1])
+            nc.sync.dma_start(out=out_view[:, first : first + width], in_=cols)
+
+        kept = D_MODEL - IN_PSUM * BANK
+        for first in range(0, STORE, BANK):
+            store(first, BANK, o_cols(first, BANK))
+        for first in range(STORE, kept, STORE):
+            store(first, STORE, o_cols(first, STORE))
+        for n in range(IN_PSUM):
+            store(kept + n * BANK, BANK, o_banks[n][:])

@@ -31,6 +31,7 @@ NORM_FLOOR = 1e-12
 WORDS = 1024
 EARLY = 8
 GU_BANKS = 8
+GRAM_DOUBLE = 2
 STEPS_AHEAD = 4
 LAG = 2
 STORE = 1024
@@ -57,15 +58,22 @@ def tile_npertokenswishglu_k_kernel(tc, x, W_gate, W_up, W_down, s_u, s_v, out):
         down_view = W_down.rearrange("l (t p) d -> p (l t) d", p=P)
         down_raw = []
 
-        def load_down_columns(first, width):
-            nc.sync.dma_start(
-                out=down_raw[first // D_LOAD][:, :, first % D_LOAD : first % D_LOAD + width],
-                in_=down_view[:, :, first : first + width],
-            )
-
         def load_down():
+            first = len(down_raw) * D_LOAD
             down_raw.append(big.tile([P, PACK, D_LOAD], BF16, tag="big", name="down_raw"))
-            load_down_columns((len(down_raw) - 1) * D_LOAD, D_LOAD)
+            nc.sync.dma_start(out=down_raw[-1][:], in_=down_view[:, :, first : first + D_LOAD])
+
+        def load_down_block(b):
+            nc.sync.dma_start(out=first_raw[:, b], in_=down_view[:, :, b * BANK : (b + 1) * BANK])
+
+        def down_block(b, words=False):
+            whole = down_raw[b // D_PER_LOAD][:]
+            whole = whole.bitcast(F32) if words else whole
+            if b < D_PER_LOAD:
+                return whole[:, b]
+            width = BANK // 2 if words else BANK
+            first = b % D_PER_LOAD * width
+            return whole[:, :, first : first + width]
 
         x_view = x.rearrange("b l d -> b (l d)")
 
@@ -76,23 +84,25 @@ def tile_npertokenswishglu_k_kernel(tc, x, W_gate, W_up, W_down, s_u, s_v, out):
         gu_raw = [[], []]
 
         def load_gate_or_up(which):
-            view = (W_gate, W_up)[which].rearrange("l (g p j) f -> p (l g) (j f)", p=P, j=PACK)
+            view = (W_gate, W_up)[which].rearrange("l (g u p e) f -> p (l g) u (e f)", p=P, u=2, e=2)
             raw = big.tile([P, CHUNK, PACK, HIDDEN], BF16, tag="big", name="gu_raw")
             for i in range(CHUNK):
                 nc.sync.dma_start(
-                    out=raw[:, i, :, :].rearrange("p j f -> p (j f)"),
-                    in_=view[:, len(gu_raw[which]) * CHUNK + i, :],
+                    out=raw[:, i, :, :].rearrange("p (u e) f -> p u (e f)", u=2),
+                    in_=view[:, len(gu_raw[which]) * CHUNK + i, :, :],
                 )
             gu_raw[which].append(raw)
 
-        down_raw.append(big.tile([P, PACK, D_LOAD], BF16, tag="big", name="down_raw"))
+        first_raw = big.tile([P, D_PER_LOAD, PACK, BANK], BF16, tag="big")
+        down_raw.append(first_raw)
         x_raw = big.tile([P, D_MODEL], BF16, tag="big", name="x_raw")
-        load_down_columns(0, BANK)
+        load_down_block(0)
         load_x(0)
-        load_down_columns(BANK, BANK)
+        load_down_block(1)
         for c in range(1, CHUNKS):
             load_x(c)
-        load_down_columns(2 * BANK, 2 * BANK)
+        load_down_block(2)
+        load_down_block(3)
         load_down()
         for c in range(CHUNKS):
             load_gate_or_up(0)
@@ -105,12 +115,14 @@ def tile_npertokenswishglu_k_kernel(tc, x, W_gate, W_up, W_down, s_u, s_v, out):
         make_identity(nc, ident_bf[:])
         minus_half = const.tile([P, 4], F32, tag="minus_half")
         nc.vector.memset(minus_half[:], -0.5)
+        first_silu = const.tile([P, 1], F32, tag="first_silu")
+        nc.scalar.activation(out=first_silu[:], in_=minus_half[:, 0:1], func=ACT.Silu)
         gain_rows = const.tile([P, P], BF16, tag="gain_rows")
         nc.vector.memset(gain_rows[:], 0.0)
         nc.scalar.dma_start(out=gain_rows[0:4, :], in_=s_u.rearrange("o (t c) -> (o t) c", c=P))
         nc.scalar.dma_start(out=gain_rows[4:8, :], in_=s_v.rearrange("o (t c) -> (o t) c", c=P))
 
-        x_words = x_raw[:].bitcast(F32).rearrange("b (g p u) -> b g u p", p=P, u=2)
+        x_words = x_raw[:].bitcast(F32).rearrange("b (g u p) -> b g u p", p=P, u=2)
         x_codes = const.tile([P, PASSES, TOKENS], U32, tag="x_codes", align_bytes=64)
         x_plane = const.tile([P, PASSES, TOKENS], U8, tag="x_plane", align_bytes=64)
 
@@ -141,7 +153,7 @@ def tile_npertokenswishglu_k_kernel(tc, x, W_gate, W_up, W_down, s_u, s_v, out):
         sizes = const.tile([P, 8], F32, tag="sizes")
 
         def prepare_gains():
-            gain_cols = turned_pool.tile([P, P], BF16, tag="turned")
+            gain_cols = acc_pool.tile([P, P], BF16, tag="acc", name="gain_cols")
             nc.tensor.transpose(gain_cols[:], gain_rows[:], ident_bf[:])
             gains = const.tile([P, 8], F32, tag="gains")
             nc.vector.tensor_copy(out=gains[:], in_=gain_cols[:, 0:8])
@@ -175,13 +187,13 @@ def tile_npertokenswishglu_k_kernel(tc, x, W_gate, W_up, W_down, s_u, s_v, out):
         def turn_pairs(blocks, accums):
             bank = turned_pool.tile([P, BANK], F32, tag="turned")
             for n in range(PACK):
-                nc.tensor.transpose(bank[:, n * P : (n + 1) * P], blocks[n].bitcast(F32), ident[:])
+                nc.tensor.transpose(bank[:, n * P : (n + 1) * P], blocks[n], ident[:])
             halves = bank[:].bitcast(BF16).rearrange("q (k e) -> q k e", e=2)
             for e in range(2):
                 add_up_squares(halves[:, :, e], BANK, accums[e])
 
-        def gu_columns(which, group, count, g, j):
-            return gu_raw[which][g // CHUNK][:, g % CHUNK, j, group * P : (group + count) * P]
+        def gu_columns(which, group, g, j):
+            return gu_raw[which][g // CHUNK][:, g % CHUNK, j, group * P : (group + 1) * P]
 
         def close_gu(which, group, parts):
             total = small.tile([P, 2], F32, tag="total")
@@ -203,7 +215,7 @@ def tile_npertokenswishglu_k_kernel(tc, x, W_gate, W_up, W_down, s_u, s_v, out):
             for n in range(2 * PACK):
                 nc.tensor.transpose(
                     bank[:, n * P : (n + 1) * P],
-                    gu_columns(which, group, 1, 2 * i + n // PACK, n % PACK),
+                    gu_columns(which, group, 2 * i + n // PACK, n % PACK),
                     ident_bf[:],
                 )
             sums = gu_sums[which, group][:, 0, :]
@@ -215,8 +227,10 @@ def tile_npertokenswishglu_k_kernel(tc, x, W_gate, W_up, W_down, s_u, s_v, out):
             if g == 0:
                 gu_sums[which, group] = small.tile([P, 2, PASSES], F32, tag="gu_sums", name="gu_sums")
             sums = gu_sums[which, group]
+            words = gu_raw[which][g // CHUNK][:].bitcast(F32)
+            first = group * P // 2
             turn_pairs(
-                [gu_columns(which, group, 2, g, j) for j in range(PACK)],
+                [words[:, g % CHUNK, j, first : first + P] for j in range(PACK)],
                 [sums[:, e, g : g + 1] for e in range(2)],
             )
             if g == PASSES - 1:
@@ -225,10 +239,9 @@ def tile_npertokenswishglu_k_kernel(tc, x, W_gate, W_up, W_down, s_u, s_v, out):
         def down_step(b, i):
             if i == 0:
                 down_sums[b] = small.tile([P, 4], F32, tag="down_sums", name="down_sums")
-            raw = down_raw[b // D_PER_LOAD]
-            first = (b % D_PER_LOAD) * BANK + i * 2 * P
+            words = down_block(b, words=True)
             turn_pairs(
-                [raw[:, t, first : first + 2 * P] for t in range(PACK)],
+                [words[:, t, i * P : (i + 1) * P] for t in range(PACK)],
                 [down_sums[b][:, 2 * i + e : 2 * i + e + 1] for e in range(2)],
             )
             if i == 1:
@@ -240,7 +253,7 @@ def tile_npertokenswishglu_k_kernel(tc, x, W_gate, W_up, W_down, s_u, s_v, out):
             if g == 0:
                 gram.append(acc_pool.tile([P, P], F32, tag="acc", name="gram"))
             for j in range(PACK):
-                columns = gu_columns(0, 0, 1, g, j)
+                columns = gu_columns(0, 0, g, j)
                 nc.tensor.matmul(
                     gram[0][:],
                     lhsT=columns,
@@ -275,7 +288,7 @@ def tile_npertokenswishglu_k_kernel(tc, x, W_gate, W_up, W_down, s_u, s_v, out):
         first_gu_step = len(steps)
         for i in range(GU_BANKS):
             steps.append((single_step, 0, 1, i))
-        ready[0, 0, 1] = len(steps)
+        ready[0, 0, 1] = len(steps) - LAG
         ready[0, 1, 1] = len(steps)
         for which, group in ((0, 2), (1, 0), (1, 2)):
             for g in range(PASSES):
@@ -285,11 +298,20 @@ def tile_npertokenswishglu_k_kernel(tc, x, W_gate, W_up, W_down, s_u, s_v, out):
             list_down(b)
         emitted = [0]
 
+        first_gram = first_gu_step + GU_BANKS - PASSES + GRAM_DOUBLE
+
+        def gram_at(s):
+            g = s - first_gram
+            single = PASSES - 2 * GRAM_DOUBLE
+            if g < single:
+                return range(max(g, 0), g + 1)
+            first = single + 2 * (g - single)
+            return range(first, min(first + 2, PASSES))
+
         def emit_steps(upto):
             for s in range(emitted[0], min(upto, len(steps))):
-                if first_gu_step <= s < first_gu_step + GU_BANKS:
-                    for g in range(2):
-                        gram_pass(2 * (s - first_gu_step) + g)
+                for g in gram_at(s):
+                    gram_pass(g)
                 steps[s][0](*steps[s][1:])
                 emitted[0] = s + 1
 
@@ -327,6 +349,7 @@ def tile_npertokenswishglu_k_kernel(tc, x, W_gate, W_up, W_down, s_u, s_v, out):
         plane = {}
         acc = {}
         u_scaled = const.tile([P, GROUPS, TOKENS], F32, tag="u_scaled")
+        swish = const.tile([P, GROUPS, TOKENS], F32, tag="swish")
         h_grouped = const.tile([P, TOKENS, PACK], BF16, tag="h_grouped", align_bytes=64)
         h_codes = const.tile([P, TOKENS], U32, tag="h_codes", align_bytes=64)
         h_plane = const.tile([P, TOKENS], U8, tag="h_plane", align_bytes=64)
@@ -343,12 +366,11 @@ def tile_npertokenswishglu_k_kernel(tc, x, W_gate, W_up, W_down, s_u, s_v, out):
             spread = spreads[unit_of(tiles[v])]
             if tiles[v][0] == "down":
                 b = tiles[v][1]
-                first = (b % D_PER_LOAD) * BANK
                 nc.vector.tensor_tensor(
                     out=grouped[v][:, 0 : BANK * PACK].rearrange(
                         "p (c i t) -> p c t i", i=NEAR, t=PACK
                     ),
-                    in0=down_raw[b // D_PER_LOAD][:, :, first : first + BANK].rearrange(
+                    in0=down_block(b).rearrange(
                         "p t (c i) -> p c t i", i=NEAR
                     ),
                     in1=spread[:]
@@ -423,14 +445,19 @@ def tile_npertokenswishglu_k_kernel(tc, x, W_gate, W_up, W_down, s_u, s_v, out):
                         scale=sizes[:, t : t + 1],
                     )
                 else:
-                    swish = small.tile([P, TOKENS], F32, tag="swish")
                     nc.scalar.activation(
-                        out=swish[:], in_=acc[which, t][:], func=ACT.Silu, scale=sizes[:, 4 + t : 5 + t]
-                    )
-                    nc.vector.tensor_tensor(
-                        out=h_grouped[:, :, t], in0=swish[:], in1=u_scaled[:, t, :], op=ALU.mult
+                        out=swish[:, t, :],
+                        in_=acc[which, t][:],
+                        func=ACT.Silu,
+                        scale=sizes[:, 4 + t : 5 + t],
                     )
             if v == last_gu:
+                nc.vector.tensor_tensor(
+                    out=h_grouped[:],
+                    in0=swish[:].rearrange("p t b -> p b t"),
+                    in1=u_scaled[:].rearrange("p t b -> p b t"),
+                    op=ALU.mult,
+                )
                 nc.vector.quantize_mx(
                     out=h_codes[:].bitcast(FP8X4),
                     scales=h_plane[:],
@@ -461,13 +488,10 @@ def tile_npertokenswishglu_k_kernel(tc, x, W_gate, W_up, W_down, s_u, s_v, out):
             else:
                 o_banks.append(o_bank)
 
-        emit_steps(1)
-        prepare_x(0)
-        emit_steps(ready["down", 0])
-        prepare_x(1)
+        for c in range(2):
+            emit_steps(c + 1)
+            prepare_x(c)
         emit_steps(ready["down", 0] + LAG)
-        prepare_x(2)
-        prepare_x(3)
         spreads[unit_of(tiles[0])] = spread_over_partitions(unit_of(tiles[0]))
         target = STEPS_AHEAD
         waiting = []
@@ -477,7 +501,9 @@ def tile_npertokenswishglu_k_kernel(tc, x, W_gate, W_up, W_down, s_u, s_v, out):
                 scale(v)
             if 1 <= v <= len(tiles):
                 quantise(v - 1)
-            if v == 0:
+            if v < 2:
+                prepare_x(2 + v)
+            if v == 2:
                 prepare_gains()
             if v == D_PER_LOAD or v == 2 * D_PER_LOAD:
                 load_gate_or_up(1)

@@ -33,6 +33,7 @@ EARLY = 8
 GU_BANKS = 8
 GRAM_DOUBLE = 2
 STEPS_AHEAD = 4
+GPSIMD_GROUP = 16
 LAG = 2
 STORE = 1024
 IN_PSUM = 2
@@ -326,11 +327,19 @@ def tile_npertokenswishglu_k_kernel(tc, x, W_gate, W_up, W_down, s_u, s_v, out):
         def unit_of(tile_):
             return tile_ if tile_[0] == "down" else tile_[0:3]
 
+        def spread_for_gpsimd(unit, spread):
+            width = unit[2] * P
+            first = width - unit[2] * GPSIMD_GROUP
+            copied = work.tile([P, 2 * P], F32, tag="spread_sb", name="spread_sb")
+            nc.scalar.copy(out=copied[:, first:width], in_=spread[:, first:width])
+            spreads_sb[unit] = copied
+
         def spread_over_partitions(unit):
             spread = spread_pool.tile([P, BANK], F32, tag="spread", name="spread")
             if unit[0] != "down" and unit[2] == 1:
                 factor = gu_inverse[:, unit[0], unit[1] : unit[1] + 1]
                 nc.tensor.transpose(spread[:, 0:P], factor.to_broadcast([P, P]), ident[:])
+                spread_for_gpsimd(unit, spread)
                 return spread
             if unit[0] == "down":
                 factors = down_inverse[:, unit[1], :]
@@ -341,9 +350,12 @@ def tile_npertokenswishglu_k_kernel(tc, x, W_gate, W_up, W_down, s_u, s_v, out):
                 nc.tensor.transpose(
                     by_half[:, c // 2, c % 2, :], factors[:, c : c + 1].to_broadcast([P, P]), ident[:]
                 )
+            if unit[0] != "down":
+                spread_for_gpsimd(unit, spread)
             return spread
 
         spreads = {}
+        spreads_sb = {}
         grouped = {}
         codes = {}
         plane = {}
@@ -382,20 +394,32 @@ def tile_npertokenswishglu_k_kernel(tc, x, W_gate, W_up, W_down, s_u, s_v, out):
                 return
             which, group, count, g0, passes = tiles[v]
             width = count * P
-            size = width * PACK
+            cut = width - count * GPSIMD_GROUP
+            spread_sb = spreads_sb[unit_of(tiles[v])]
+            by_pass = grouped[v][:].rearrange("p (g w j) -> p g w j", w=width, j=PACK)
+            for n in range(0, passes, CHUNK):
+                nc.gpsimd.tensor_tensor(
+                    out=by_pass[:, n : n + CHUNK, cut:width, :],
+                    in0=gu_raw[which][(g0 + n) // CHUNK][
+                        :, :, :, group * P + cut : group * P + width
+                    ].rearrange("p g j w -> p g w j"),
+                    in1=spread_sb[:, cut:width]
+                    .unsqueeze(1)
+                    .unsqueeze(3)
+                    .to_broadcast([P, CHUNK, width - cut, PACK]),
+                    op=ALU.mult,
+                )
             for n in range(passes):
                 g = g0 + n
                 nc.vector.tensor_tensor(
-                    out=grouped[v][:, n * size : (n + 1) * size].rearrange(
-                        "p (c i j) -> p c j i", i=NEAR, j=PACK
-                    ),
+                    out=by_pass[:, n, 0:cut, :].rearrange("p (c i) j -> p c j i", i=NEAR),
                     in0=gu_raw[which][g // CHUNK][
-                        :, g % CHUNK, :, group * P : group * P + width
+                        :, g % CHUNK, :, group * P : group * P + cut
                     ].rearrange("p j (c i) -> p c j i", i=NEAR),
-                    in1=spread[:, 0:width]
+                    in1=spread[:, 0:cut]
                     .rearrange("p (c i) -> p c i", i=NEAR)
                     .unsqueeze(2)
-                    .to_broadcast([P, width // NEAR, PACK, NEAR]),
+                    .to_broadcast([P, cut // NEAR, PACK, NEAR]),
                     op=ALU.mult,
                 )
 

@@ -31,12 +31,12 @@ NORM_FLOOR = 1e-12
 WORDS = 1024
 EARLY = 8
 GU_BANKS = 8
-GRAM_DOUBLE = 2
+FIRST_GRAM = 8
 STEPS_AHEAD = 4
+LATE = BLOCKS - EARLY
 GPSIMD_GROUP = 16
+GPSIMD_DOWN = 64
 LAG = 2
-STORE = 1024
-IN_PSUM = 2
 
 FLOPS = 3 * 2 * TOKENS * D_MODEL * HIDDEN
 
@@ -47,8 +47,7 @@ def tile_npertokenswishglu_k_kernel(tc, x, W_gate, W_up, W_down, s_u, s_v, out):
         const = ctx.enter_context(tc.tile_pool(name="const", bufs=1))
         big = ctx.enter_context(tc.tile_pool(name="big", bufs=9))
         work = ctx.enter_context(tc.tile_pool(name="work", bufs=3))
-        packed = ctx.enter_context(tc.tile_pool(name="packed", bufs=4))
-        early = ctx.enter_context(tc.tile_pool(name="early", bufs=EARLY))
+        packed = ctx.enter_context(tc.tile_pool(name="packed", bufs=3))
         junk = ctx.enter_context(tc.tile_pool(name="junk", bufs=2))
         small = ctx.enter_context(tc.tile_pool(name="small", bufs=4))
         turned_pool = ctx.enter_context(tc.psum_pool(name="turned_pool", bufs=3))
@@ -61,7 +60,7 @@ def tile_npertokenswishglu_k_kernel(tc, x, W_gate, W_up, W_down, s_u, s_v, out):
 
         def load_down():
             first = len(down_raw) * D_LOAD
-            down_raw.append(big.tile([P, PACK, D_LOAD], BF16, tag="big", name="down_raw"))
+            down_raw.append(big.tile([P, PACK, D_LOAD], BF16, tag="big", align_bytes=64, name="down_raw"))
             nc.sync.dma_start(out=down_raw[-1][:], in_=down_view[:, :, first : first + D_LOAD])
 
         def load_down_block(b):
@@ -86,7 +85,7 @@ def tile_npertokenswishglu_k_kernel(tc, x, W_gate, W_up, W_down, s_u, s_v, out):
 
         def load_gate_or_up(which):
             view = (W_gate, W_up)[which].rearrange("l (g u p e) f -> p (l g) u (e f)", p=P, u=2, e=2)
-            raw = big.tile([P, CHUNK, PACK, HIDDEN], BF16, tag="big", name="gu_raw")
+            raw = big.tile([P, CHUNK, PACK, HIDDEN], BF16, tag="big", align_bytes=64, name="gu_raw")
             for i in range(CHUNK):
                 nc.sync.dma_start(
                     out=raw[:, i, :, :].rearrange("p (u e) f -> p u (e f)", u=2),
@@ -94,9 +93,9 @@ def tile_npertokenswishglu_k_kernel(tc, x, W_gate, W_up, W_down, s_u, s_v, out):
                 )
             gu_raw[which].append(raw)
 
-        first_raw = big.tile([P, D_PER_LOAD, PACK, BANK], BF16, tag="big")
+        first_raw = big.tile([P, D_PER_LOAD, PACK, BANK], BF16, tag="big", align_bytes=64)
         down_raw.append(first_raw)
-        x_raw = big.tile([P, D_MODEL], BF16, tag="big", name="x_raw")
+        x_raw = big.tile([P, D_MODEL], BF16, tag="big", align_bytes=64, name="x_raw")
         load_down_block(0)
         load_x(0)
         load_down_block(1)
@@ -289,7 +288,7 @@ def tile_npertokenswishglu_k_kernel(tc, x, W_gate, W_up, W_down, s_u, s_v, out):
         first_gu_step = len(steps)
         for i in range(GU_BANKS):
             steps.append((single_step, 0, 1, i))
-        ready[0, 0, 1] = len(steps) - LAG
+        ready[0, 0, 1] = FIRST_GRAM + PASSES - LAG
         ready[0, 1, 1] = len(steps)
         for which, group in ((0, 2), (1, 0), (1, 2)):
             for g in range(PASSES):
@@ -299,20 +298,10 @@ def tile_npertokenswishglu_k_kernel(tc, x, W_gate, W_up, W_down, s_u, s_v, out):
             list_down(b)
         emitted = [0]
 
-        first_gram = first_gu_step + GU_BANKS - PASSES + GRAM_DOUBLE
-
-        def gram_at(s):
-            g = s - first_gram
-            single = PASSES - 2 * GRAM_DOUBLE
-            if g < single:
-                return range(max(g, 0), g + 1)
-            first = single + 2 * (g - single)
-            return range(first, min(first + 2, PASSES))
-
         def emit_steps(upto):
             for s in range(emitted[0], min(upto, len(steps))):
-                for g in gram_at(s):
-                    gram_pass(g)
+                if FIRST_GRAM <= s < FIRST_GRAM + PASSES:
+                    gram_pass(s - FIRST_GRAM)
                 steps[s][0](*steps[s][1:])
                 emitted[0] = s + 1
 
@@ -327,10 +316,17 @@ def tile_npertokenswishglu_k_kernel(tc, x, W_gate, W_up, W_down, s_u, s_v, out):
         def unit_of(tile_):
             return tile_ if tile_[0] == "down" else tile_[0:3]
 
+        def gpsimd_columns(unit):
+            if unit[0] == "down":
+                return GPSIMD_DOWN if unit[1] >= EARLY else 0
+            return unit[2] * GPSIMD_GROUP
+
         def spread_for_gpsimd(unit, spread):
-            width = unit[2] * P
-            first = width - unit[2] * GPSIMD_GROUP
-            copied = work.tile([P, 2 * P], F32, tag="spread_sb", name="spread_sb")
+            if gpsimd_columns(unit) == 0:
+                return
+            width = BANK if unit[0] == "down" else unit[2] * P
+            first = width - gpsimd_columns(unit)
+            copied = work.tile([P, BANK], F32, tag="spread_sb", name="spread_sb")
             nc.scalar.copy(out=copied[:, first:width], in_=spread[:, first:width])
             spreads_sb[unit] = copied
 
@@ -350,8 +346,7 @@ def tile_npertokenswishglu_k_kernel(tc, x, W_gate, W_up, W_down, s_u, s_v, out):
                 nc.tensor.transpose(
                     by_half[:, c // 2, c % 2, :], factors[:, c : c + 1].to_broadcast([P, P]), ident[:]
                 )
-            if unit[0] != "down":
-                spread_for_gpsimd(unit, spread)
+            spread_for_gpsimd(unit, spread)
             return spread
 
         spreads = {}
@@ -360,41 +355,43 @@ def tile_npertokenswishglu_k_kernel(tc, x, W_gate, W_up, W_down, s_u, s_v, out):
         codes = {}
         plane = {}
         acc = {}
+        down_codes = [const.tile([P, EARLY, BANK], U32, tag="early_codes", align_bytes=64, name="early_codes")]
+        down_plane = const.tile([P, BLOCKS, BANK], U8, tag="down_plane", align_bytes=64)
         u_scaled = const.tile([P, GROUPS, TOKENS], F32, tag="u_scaled")
         swish = const.tile([P, GROUPS, TOKENS], F32, tag="swish")
         h_grouped = const.tile([P, TOKENS, PACK], BF16, tag="h_grouped", align_bytes=64)
         h_codes = const.tile([P, TOKENS], U32, tag="h_codes", align_bytes=64)
         h_plane = const.tile([P, TOKENS], U8, tag="h_plane", align_bytes=64)
-        o_sb = []
-        o_banks = []
         o_squares = const.tile([P, BLOCKS], F32, tag="o_squares")
-
-        def o_cols(first, width):
-            half = D_MODEL // 2
-            return o_sb[first // half][:, first % half : first % half + width]
 
         def scale(v):
             grouped[v] = work.tile([P, WORDS * PACK], BF16, tag="grouped", align_bytes=64, name="grouped")
             spread = spreads[unit_of(tiles[v])]
             if tiles[v][0] == "down":
                 b = tiles[v][1]
+                cut = BANK - gpsimd_columns(unit_of(tiles[v]))
                 nc.vector.tensor_tensor(
-                    out=grouped[v][:, 0 : BANK * PACK].rearrange(
-                        "p (c i t) -> p c t i", i=NEAR, t=PACK
-                    ),
-                    in0=down_block(b).rearrange(
-                        "p t (c i) -> p c t i", i=NEAR
-                    ),
-                    in1=spread[:]
+                    out=grouped[v][:, 0 : cut * PACK].rearrange("p (c i t) -> p c t i", i=NEAR, t=PACK),
+                    in0=down_block(b)[:, :, 0:cut].rearrange("p t (c i) -> p c t i", i=NEAR),
+                    in1=spread[:, 0:cut]
                     .rearrange("p (c i) -> p c i", i=NEAR)
                     .unsqueeze(2)
-                    .to_broadcast([P, BANK // NEAR, PACK, NEAR]),
+                    .to_broadcast([P, cut // NEAR, PACK, NEAR]),
                     op=ALU.mult,
                 )
+                if cut < BANK:
+                    nc.gpsimd.tensor_tensor(
+                        out=grouped[v][:, cut * PACK : BANK * PACK].rearrange("p (w t) -> p w t", t=PACK),
+                        in0=down_block(b)[:, :, cut:BANK].rearrange("p t w -> p w t"),
+                        in1=spreads_sb[unit_of(tiles[v])][:, cut:BANK]
+                        .unsqueeze(2)
+                        .to_broadcast([P, BANK - cut, PACK]),
+                        op=ALU.mult,
+                    )
                 return
             which, group, count, g0, passes = tiles[v]
             width = count * P
-            cut = width - count * GPSIMD_GROUP
+            cut = width - gpsimd_columns(unit_of(tiles[v]))
             spread_sb = spreads_sb[unit_of(tiles[v])]
             by_pass = grouped[v][:].rearrange("p (g w j) -> p g w j", w=width, j=PACK)
             for n in range(0, passes, CHUNK):
@@ -424,19 +421,20 @@ def tile_npertokenswishglu_k_kernel(tc, x, W_gate, W_up, W_down, s_u, s_v, out):
                 )
 
         def quantise(v):
-            is_early = v < EARLY
-            words = BANK if tiles[v][0] == "down" else WORDS
-            if is_early:
-                codes[v] = early.tile([P, BANK], U32, tag="early_codes", align_bytes=64, name="early_codes")
-                plane[v] = early.tile([P, BANK], U8, tag="early_plane", align_bytes=64, name="early_plane")
+            if tiles[v][0] == "down":
+                b = tiles[v][1]
+                if b == EARLY:
+                    down_codes.append(
+                        big.tile([P, LATE, BANK], U32, tag="big", align_bytes=64, name="late_codes")
+                    )
+                codes[v] = down_codes[b // EARLY][:, b % EARLY, :]
+                plane[v] = down_plane[:, b, :]
+                source = grouped[v][:, 0 : BANK * PACK]
             else:
-                codes[v] = packed.tile([P, WORDS], U32, tag="codes", align_bytes=64, name="codes")
-                plane[v] = packed.tile([P, WORDS], U8, tag="plane", align_bytes=64, name="plane")
-            nc.vector.quantize_mx(
-                out=codes[v][:, 0:words].bitcast(FP8X4),
-                scales=plane[v][:, 0:words],
-                in_=grouped[v][:, 0 : words * PACK],
-            )
+                codes[v] = packed.tile([P, WORDS], U32, tag="codes", align_bytes=64, name="codes")[:]
+                plane[v] = packed.tile([P, WORDS], U8, tag="plane", align_bytes=64, name="plane")[:]
+                source = grouped[v][:]
+            nc.vector.quantize_mx(out=codes[v].bitcast(FP8X4), scales=plane[v], in_=source)
 
         def multiply_gate_up(v):
             which, group, count, g0, passes = tiles[v]
@@ -488,29 +486,25 @@ def tile_npertokenswishglu_k_kernel(tc, x, W_gate, W_up, W_down, s_u, s_v, out):
                     in_=h_grouped[:].rearrange("p b t -> p (b t)"),
                 )
 
-        def multiply_down(v):
-            b = tiles[v][1]
-            if not o_sb:
-                for i in range(2):
-                    o_sb.append(big.tile([P, D_MODEL // 2], F32, tag="big", name="o_sb"))
+        def multiply_down(b):
             o_bank = acc_pool.tile([P, BANK], F32, tag="acc", name="o_bank")
             nc.tensor.matmul_mx(
                 out=o_bank[:],
                 lhsT=h_codes[:].bitcast(FP8X4),
                 lhsT_scale=h_plane[:],
-                rhs=codes[v][:, 0:BANK].bitcast(FP8X4),
-                rhs_scale=plane[v][:, 0:BANK],
+                rhs=down_codes[b // EARLY][:, b % EARLY, :].bitcast(FP8X4),
+                rhs_scale=down_plane[:, b, :],
                 start=True,
                 stop=True,
             )
+            return o_bank
+
+        def square_down(b):
+            o_bank = multiply_down(b)
             squares = junk.tile([P, 2 * BANK], BF16, tag="squares")
             nc.scalar.activation(
                 out=squares[:, 0:BANK], in_=o_bank[:], func=ACT.Square, accum_out=o_squares[:, b : b + 1]
             )
-            if b < BLOCKS - IN_PSUM:
-                nc.scalar.copy(out=o_cols(b * BANK, BANK), in_=o_bank[:])
-            else:
-                o_banks.append(o_bank)
 
         for c in range(2):
             emit_steps(c + 1)
@@ -518,8 +512,7 @@ def tile_npertokenswishglu_k_kernel(tc, x, W_gate, W_up, W_down, s_u, s_v, out):
         emit_steps(ready["down", 0] + LAG)
         spreads[unit_of(tiles[0])] = spread_over_partitions(unit_of(tiles[0]))
         target = STEPS_AHEAD
-        waiting = []
-        multiplied = 0
+        squared = 0
         for v in range(len(tiles) + 2):
             if v < len(tiles):
                 scale(v)
@@ -541,15 +534,13 @@ def tile_npertokenswishglu_k_kernel(tc, x, W_gate, W_up, W_down, s_u, s_v, out):
                 spreads[unit] = spread_over_partitions(unit)
             target = target + (3 if v < EARLY else 4)
             emit_steps(target)
-            if v >= 2:
-                if tiles[v - 2][0] == "down":
-                    waiting.append(v - 2)
-                else:
-                    multiply_gate_up(v - 2)
+            if EARLY <= v - 2 <= last_gu:
+                multiply_gate_up(v - 2)
             if v - 2 > last_gu:
-                for w in waiting[multiplied : multiplied + 3]:
-                    multiply_down(w)
-                    multiplied = multiplied + 1
+                square_down(tiles[v - 2][1])
+                for b in range(squared, min(squared + 2, EARLY)):
+                    square_down(b)
+                    squared = b + 1
 
         o_total = small.tile([P, 1], F32, tag="o_total")
         o_copied = small.tile([P, BLOCKS], F32, tag="o_copied")
@@ -557,16 +548,20 @@ def tile_npertokenswishglu_k_kernel(tc, x, W_gate, W_up, W_down, s_u, s_v, out):
         o_inverse = small.tile([P, 1], F32, tag="o_inverse")
         one_over_norm(o_inverse[:], o_total[:], 1)
         out_view = out.rearrange("b l d -> b (l d)")
-
-        def store(first, width, source):
-            cols = o_cols(first, width)
-            nc.vector.tensor_scalar_mul(out=cols, in0=source, scalar1=o_inverse[:, 0:1])
-            nc.sync.dma_start(out=out_view[:, first : first + width], in_=cols)
-
-        kept = D_MODEL - IN_PSUM * BANK
-        for first in range(0, STORE, BANK):
-            store(first, BANK, o_cols(first, BANK))
-        for first in range(STORE, kept, STORE):
-            store(first, STORE, o_cols(first, STORE))
-        for n in range(IN_PSUM):
-            store(kept + n * BANK, BANK, o_banks[n][:])
+        o_sb = [big.tile([P, D_MODEL // 2], F32, tag="big", align_bytes=64, name="o_sb") for n in range(2)]
+        for b in range(BLOCKS):
+            half = o_sb[b // (BLOCKS // 2)]
+            first = (b % (BLOCKS // 2)) * BANK
+            o_bank = multiply_down(b)
+            if b % 2 == 0:
+                nc.vector.tensor_scalar_mul(
+                    out=half[:, first : first + BANK], in0=o_bank[:], scalar1=o_inverse[:, 0:1]
+                )
+            else:
+                nc.scalar.activation(
+                    out=half[:, first : first + BANK], in_=o_bank[:], func=ACT.Copy, scale=o_inverse[:, 0:1]
+                )
+                nc.sync.dma_start(
+                    out=out_view[:, (b - 1) * BANK : (b + 1) * BANK],
+                    in_=half[:, first - BANK : first + BANK],
+                )

import math
from contextlib import ExitStack

import concourse.mybir as mybir
from concourse.masks import make_identity

F32 = mybir.dt.float32
BF16 = mybir.dt.bfloat16
U32 = mybir.dt.uint32
U8 = mybir.dt.uint8
FP8X4 = mybir.dt.float8_e4m3fn_x4
ACT = mybir.ActivationFunctionType
ALU = mybir.AluOpType

P = 128
NEAR = 4
PACK = 4
K_PASS = P * PACK
TOKENS = 128
D_MODEL = 8192
HIDDEN = 512
GROUPS = HIDDEN // P
PASSES = D_MODEL // K_PASS
CHUNK = 4
CHUNKS = PASSES // CHUNK
BANK = 512
BLOCKS = D_MODEL // BANK
D_LOAD = 2048
D_PER_LOAD = D_LOAD // BANK
NORM_FLOOR = 1e-12
WORDS = 1024
EARLY = 8
GU_BANKS = 8
FIRST_GRAM = 8
STEPS_AHEAD = 4
LATE = BLOCKS - EARLY
GPSIMD_GROUP = 16
GPSIMD_DOWN = 64
LAG = 2

FLOPS = 3 * 2 * TOKENS * D_MODEL * HIDDEN


def tile_npertokenswishglu_k_kernel(tc, x, W_gate, W_up, W_down, s_u, s_v, out):
    nc = tc.nc
    with ExitStack() as ctx:
        const = ctx.enter_context(tc.tile_pool(name="const", bufs=1))
        big = ctx.enter_context(tc.tile_pool(name="big", bufs=9))
        work = ctx.enter_context(tc.tile_pool(name="work", bufs=3))
        packed = ctx.enter_context(tc.tile_pool(name="packed", bufs=3))
        junk = ctx.enter_context(tc.tile_pool(name="junk", bufs=2))
        small = ctx.enter_context(tc.tile_pool(name="small", bufs=4))
        turned_pool = ctx.enter_context(tc.psum_pool(name="turned_pool", bufs=3))
        spread_pool = ctx.enter_context(tc.psum_pool(name="spread_pool", bufs=2))
        acc_pool = ctx.enter_context(tc.psum_pool(name="acc_pool", bufs=3))
        ctx.enter_context(tc.manual_schedule())

        down_view = W_down.rearrange("l (t p) d -> p (l t) d", p=P)
        down_raw = []

        def load_down():
            first = len(down_raw) * D_LOAD
            down_raw.append(big.tile([P, PACK, D_LOAD], BF16, tag="big", align_bytes=64, name="down_raw"))
            nc.sync.dma_start(out=down_raw[-1][:], in_=down_view[:, :, first : first + D_LOAD])

        def load_down_block(b):
            nc.sync.dma_start(out=first_raw[:, b], in_=down_view[:, :, b * BANK : (b + 1) * BANK])

        def down_block(b, words=False):
            whole = down_raw[b // D_PER_LOAD][:]
            whole = whole.bitcast(F32) if words else whole
            if b < D_PER_LOAD:
                return whole[:, b]
            width = BANK // 2 if words else BANK
            first = b % D_PER_LOAD * width
            return whole[:, :, first : first + width]

        x_view = x.rearrange("b l d -> b (l d)")

        def load_x(c):
            cols = slice(c * CHUNK * K_PASS, (c + 1) * CHUNK * K_PASS)
            nc.sync.dma_start(out=x_raw[:, cols], in_=x_view[:, cols])

        gu_raw = [[], []]

        def load_gate_or_up(which):
            view = (W_gate, W_up)[which].rearrange("l (g u p e) f -> p (l g) u (e f)", p=P, u=2, e=2)
            raw = big.tile([P, CHUNK, PACK, HIDDEN], BF16, tag="big", align_bytes=64, name="gu_raw")
            for i in range(CHUNK):
                nc.sync.dma_start(
                    out=raw[:, i, :, :].rearrange("p (u e) f -> p u (e f)", u=2),
                    in_=view[:, len(gu_raw[which]) * CHUNK + i, :, :],
                )
            gu_raw[which].append(raw)

        first_raw = big.tile([P, D_PER_LOAD, PACK, BANK], BF16, tag="big", align_bytes=64)
        down_raw.append(first_raw)
        x_raw = big.tile([P, D_MODEL], BF16, tag="big", align_bytes=64, name="x_raw")
        load_down_block(0)
        load_x(0)
        load_down_block(1)
        for c in range(1, CHUNKS):
            load_x(c)
        load_down_block(2)
        load_down_block(3)
        load_down()
        for c in range(CHUNKS):
            load_gate_or_up(0)
        for c in range(2):
            load_gate_or_up(1)

        ident = const.tile([P, P], F32, tag="ident")
        make_identity(nc, ident[:])
        ident_bf = const.tile([P, P], BF16, tag="ident_bf")
        make_identity(nc, ident_bf[:])
        minus_half = const.tile([P, 4], F32, tag="minus_half")
        nc.vector.memset(minus_half[:], -0.5)
        first_silu = const.tile([P, 1], F32, tag="first_silu")
        nc.scalar.activation(out=first_silu[:], in_=minus_half[:, 0:1], func=ACT.Silu)
        gain_rows = const.tile([P, P], BF16, tag="gain_rows")
        nc.vector.memset(gain_rows[:], 0.0)
        nc.scalar.dma_start(out=gain_rows[0:4, :], in_=s_u.rearrange("o (t c) -> (o t) c", c=P))
        nc.scalar.dma_start(out=gain_rows[4:8, :], in_=s_v.rearrange("o (t c) -> (o t) c", c=P))

        x_words = x_raw[:].bitcast(F32).rearrange("b (g u p) -> b g u p", p=P, u=2)
        x_codes = const.tile([P, PASSES, TOKENS], U32, tag="x_codes", align_bytes=64)
        x_plane = const.tile([P, PASSES, TOKENS], U8, tag="x_plane", align_bytes=64)

        def prepare_x(c):
            x_grouped = work.tile([P, CHUNK, TOKENS * PACK], BF16, tag="grouped", align_bytes=64)
            x_grouped_words = x_grouped[:].bitcast(F32)
            for h in range(2):
                bank = turned_pool.tile([P, BANK], F32, tag="turned")
                for i in range(2):
                    for u in range(2):
                        col = (2 * i + u) * P
                        nc.tensor.transpose(
                            bank[:, col : col + P], x_words[:, c * CHUNK + 2 * h + i, u, :], ident[:]
                        )
                nc.vector.tensor_copy(
                    out=x_grouped_words[:, 2 * h : 2 * h + 2, :].rearrange(
                        "p i (b u) -> p i b u", u=2
                    ),
                    in_=bank[:].rearrange("p (i u b) -> p i b u", i=2, u=2),
                )
            passes = slice(c * CHUNK, (c + 1) * CHUNK)
            nc.vector.quantize_mx(
                out=x_codes[:, passes, :].rearrange("p g b -> p (g b)").bitcast(FP8X4),
                scales=x_plane[:, passes, :].rearrange("p g b -> p (g b)"),
                in_=x_grouped[:].rearrange("p g n -> p (g n)"),
            )

        sizes = const.tile([P, 8], F32, tag="sizes")

        def prepare_gains():
            gain_cols = acc_pool.tile([P, P], BF16, tag="acc", name="gain_cols")
            nc.tensor.transpose(gain_cols[:], gain_rows[:], ident_bf[:])
            gains = const.tile([P, 8], F32, tag="gains")
            nc.vector.tensor_copy(out=gains[:], in_=gain_cols[:, 0:8])
            nc.vector.scalar_tensor_tensor(
                out=sizes[:], in0=gains[:], scalar=-1.0, in1=gains[:], op0=ALU.mult, op1=ALU.max
            )
            nc.vector.tensor_scalar_mul(
                out=sizes[:, 4:8], in0=sizes[:, 4:8], scalar1=math.sqrt(float(D_MODEL))
            )

        gu_inverse = const.tile([P, 2, GROUPS], F32, tag="gu_inverse")
        down_inverse = const.tile([P, BLOCKS, 4], F32, tag="down_inverse")
        gu_sums = {}
        down_sums = {}

        def one_over_norm(inverse, sum_of_squares, width):
            floored = small.tile([P, width], F32, tag="floored")
            nc.gpsimd.tensor_scalar_max(
                out=floored[:], in0=sum_of_squares, scalar1=NORM_FLOOR * NORM_FLOOR
            )
            nc.gpsimd.tensor_tensor(
                out=inverse, in0=floored[:], in1=minus_half[:, 0:width], op=ALU.pow
            )

        def add_up_squares(turned, width, accum):
            squares = junk.tile([P, 2 * BANK], BF16, tag="squares")
            nc.scalar.activation(
                out=squares[:, 0:width], in_=turned, func=ACT.Square, accum_out=accum
            )

        def turn_pairs(blocks, accums):
            bank = turned_pool.tile([P, BANK], F32, tag="turned")
            for n in range(PACK):
                nc.tensor.transpose(bank[:, n * P : (n + 1) * P], blocks[n], ident[:])
            halves = bank[:].bitcast(BF16).rearrange("q (k e) -> q k e", e=2)
            for e in range(2):
                add_up_squares(halves[:, :, e], BANK, accums[e])

        def gu_columns(which, group, g, j):
            return gu_raw[which][g // CHUNK][:, g % CHUNK, j, group * P : (group + 1) * P]

        def close_gu(which, group, parts):
            total = small.tile([P, 2], F32, tag="total")
            for e in range(len(parts)):
                copied = small.tile([P, PASSES], F32, tag="copied")
                nc.scalar.activation(
                    out=copied[:, 0 : parts[e].shape[1]],
                    in_=parts[e],
                    func=ACT.Copy,
                    accum_out=total[:, e : e + 1],
                )
            width = len(parts)
            one_over_norm(gu_inverse[:, which, group : group + width], total[:, 0:width], width)

        def single_step(which, group, i):
            if i == 0:
                gu_sums[which, group] = small.tile([P, 2, PASSES], F32, tag="gu_sums", name="gu_sums")
            bank = turned_pool.tile([P, 2 * BANK], BF16, tag="turned")
            for n in range(2 * PACK):
                nc.tensor.transpose(
                    bank[:, n * P : (n + 1) * P],
                    gu_columns(which, group, 2 * i + n // PACK, n % PACK),
                    ident_bf[:],
                )
            sums = gu_sums[which, group][:, 0, :]
            add_up_squares(bank[:], 2 * BANK, sums[:, i : i + 1])
            if i == GU_BANKS - 1:
                close_gu(which, group, [sums[:, 0:GU_BANKS]])

        def pair_step(which, group, g):
            if g == 0:
                gu_sums[which, group] = small.tile([P, 2, PASSES], F32, tag="gu_sums", name="gu_sums")
            sums = gu_sums[which, group]
            words = gu_raw[which][g // CHUNK][:].bitcast(F32)
            first = group * P // 2
            turn_pairs(
                [words[:, g % CHUNK, j, first : first + P] for j in range(PACK)],
                [sums[:, e, g : g + 1] for e in range(2)],
            )
            if g == PASSES - 1:
                close_gu(which, group, [sums[:, e, :] for e in range(2)])

        def down_step(b, i):
            if i == 0:
                down_sums[b] = small.tile([P, 4], F32, tag="down_sums", name="down_sums")
            words = down_block(b, words=True)
            turn_pairs(
                [words[:, t, i * P : (i + 1) * P] for t in range(PACK)],
                [down_sums[b][:, 2 * i + e : 2 * i + e + 1] for e in range(2)],
            )
            if i == 1:
                one_over_norm(down_inverse[:, b, :], down_sums[b][:], 4)

        gram = []

        def gram_pass(g):
            if g == 0:
                gram.append(acc_pool.tile([P, P], F32, tag="acc", name="gram"))
            for j in range(PACK):
                columns = gu_columns(0, 0, g, j)
                nc.tensor.matmul(
                    gram[0][:],
                    lhsT=columns,
                    rhs=columns,
                    start=(g == 0 and j == 0),
                    stop=(g == PASSES - 1 and j == PACK - 1),
                )
            if g == PASSES - 1:
                diagonal = const.tile([P, P], F32, tag="diagonal")
                total = small.tile([P, 1], F32, tag="total")
                nc.vector.scalar_tensor_tensor(
                    out=diagonal[:],
                    in0=gram[0][:],
                    scalar=1.0,
                    in1=ident[:],
                    op0=ALU.mult,
                    op1=ALU.mult,
                    accum_out=total[:],
                )
                one_over_norm(gu_inverse[:, 0, 0:1], total[:], 1)

        steps = []
        ready = {}

        def list_down(b):
            for i in range(2):
                steps.append((down_step, b, i))
            ready["down", b] = len(steps)

        for b in range(EARLY):
            list_down(b)
        first_gu_step = len(steps)
        for i in range(GU_BANKS):
            steps.append((single_step, 0, 1, i))
        ready[0, 0, 1] = FIRST_GRAM + PASSES - LAG
        ready[0, 1, 1] = len(steps)
        for which, group in ((0, 2), (1, 0), (1, 2)):
            for g in range(PASSES):
                steps.append((pair_step, which, group, g))
            ready[which, group, 2] = len(steps)
        for b in range(EARLY, BLOCKS):
            list_down(b)
        emitted = [0]

        def emit_steps(upto):
            for s in range(emitted[0], min(upto, len(steps))):
                if FIRST_GRAM <= s < FIRST_GRAM + PASSES:
                    gram_pass(s - FIRST_GRAM)
                steps[s][0](*steps[s][1:])
                emitted[0] = s + 1

        tiles = [("down", b) for b in range(EARLY)]
        for which, group, count in ((0, 0, 1), (0, 1, 1), (0, 2, 2), (1, 0, 2), (1, 2, 2)):
            passes = WORDS // (count * P)
            for g in range(0, PASSES, passes):
                tiles.append((which, group, count, g, passes))
        last_gu = len(tiles) - 1
        tiles = tiles + [("down", b) for b in range(EARLY, BLOCKS)]

        def unit_of(tile_):
            return tile_ if tile_[0] == "down" else tile_[0:3]

        def gpsimd_columns(unit):
            if unit[0] == "down":
                return GPSIMD_DOWN if unit[1] >= EARLY else 0
            return unit[2] * GPSIMD_GROUP

        def spread_for_gpsimd(unit, spread):
            if gpsimd_columns(unit) == 0:
                return
            width = BANK if unit[0] == "down" else unit[2] * P
            first = width - gpsimd_columns(unit)
            copied = work.tile([P, BANK], F32, tag="spread_sb", name="spread_sb")
            nc.scalar.copy(out=copied[:, first:width], in_=spread[:, first:width])
            spreads_sb[unit] = copied

        def spread_over_partitions(unit):
            spread = spread_pool.tile([P, BANK], F32, tag="spread", name="spread")
            if unit[0] != "down" and unit[2] == 1:
                factor = gu_inverse[:, unit[0], unit[1] : unit[1] + 1]
                nc.tensor.transpose(spread[:, 0:P], factor.to_broadcast([P, P]), ident[:])
                spread_for_gpsimd(unit, spread)
                return spread
            if unit[0] == "down":
                factors = down_inverse[:, unit[1], :]
            else:
                factors = gu_inverse[:, unit[0], unit[1] : unit[1] + 2]
            by_half = spread[:].rearrange("p (n q e) -> p n e q", q=P, e=2)
            for c in range(factors.shape[1]):
                nc.tensor.transpose(
                    by_half[:, c // 2, c % 2, :], factors[:, c : c + 1].to_broadcast([P, P]), ident[:]
                )
            spread_for_gpsimd(unit, spread)
            return spread

        spreads = {}
        spreads_sb = {}
        grouped = {}
        codes = {}
        plane = {}
        acc = {}
        down_codes = [const.tile([P, EARLY, BANK], U32, tag="early_codes", align_bytes=64, name="early_codes")]
        down_plane = const.tile([P, BLOCKS, BANK], U8, tag="down_plane", align_bytes=64)
        u_scaled = const.tile([P, GROUPS, TOKENS], F32, tag="u_scaled")
        swish = const.tile([P, GROUPS, TOKENS], F32, tag="swish")
        h_grouped = const.tile([P, TOKENS, PACK], BF16, tag="h_grouped", align_bytes=64)
        h_codes = const.tile([P, TOKENS], U32, tag="h_codes", align_bytes=64)
        h_plane = const.tile([P, TOKENS], U8, tag="h_plane", align_bytes=64)
        o_squares = const.tile([P, BLOCKS], F32, tag="o_squares")

        def scale(v):
            grouped[v] = work.tile([P, WORDS * PACK], BF16, tag="grouped", align_bytes=64, name="grouped")
            spread = spreads[unit_of(tiles[v])]
            if tiles[v][0] == "down":
                b = tiles[v][1]
                cut = BANK - gpsimd_columns(unit_of(tiles[v]))
                nc.vector.tensor_tensor(
                    out=grouped[v][:, 0 : cut * PACK].rearrange("p (c i t) -> p c t i", i=NEAR, t=PACK),
                    in0=down_block(b)[:, :, 0:cut].rearrange("p t (c i) -> p c t i", i=NEAR),
                    in1=spread[:, 0:cut]
                    .rearrange("p (c i) -> p c i", i=NEAR)
                    .unsqueeze(2)
                    .to_broadcast([P, cut // NEAR, PACK, NEAR]),
                    op=ALU.mult,
                )
                if cut < BANK:
                    nc.gpsimd.tensor_tensor(
                        out=grouped[v][:, cut * PACK : BANK * PACK].rearrange("p (w t) -> p w t", t=PACK),
                        in0=down_block(b)[:, :, cut:BANK].rearrange("p t w -> p w t"),
                        in1=spreads_sb[unit_of(tiles[v])][:, cut:BANK]
                        .unsqueeze(2)
                        .to_broadcast([P, BANK - cut, PACK]),
                        op=ALU.mult,
                    )
                return
            which, group, count, g0, passes = tiles[v]
            width = count * P
            cut = width - gpsimd_columns(unit_of(tiles[v]))
            spread_sb = spreads_sb[unit_of(tiles[v])]
            by_pass = grouped[v][:].rearrange("p (g w j) -> p g w j", w=width, j=PACK)
            for n in range(0, passes, CHUNK):
                nc.gpsimd.tensor_tensor(
                    out=by_pass[:, n : n + CHUNK, cut:width, :],
                    in0=gu_raw[which][(g0 + n) // CHUNK][
                        :, :, :, group * P + cut : group * P + width
                    ].rearrange("p g j w -> p g w j"),
                    in1=spread_sb[:, cut:width]
                    .unsqueeze(1)
                    .unsqueeze(3)
                    .to_broadcast([P, CHUNK, width - cut, PACK]),
                    op=ALU.mult,
                )
            for n in range(passes):
                g = g0 + n
                nc.vector.tensor_tensor(
                    out=by_pass[:, n, 0:cut, :].rearrange("p (c i) j -> p c j i", i=NEAR),
                    in0=gu_raw[which][g // CHUNK][
                        :, g % CHUNK, :, group * P : group * P + cut
                    ].rearrange("p j (c i) -> p c j i", i=NEAR),
                    in1=spread[:, 0:cut]
                    .rearrange("p (c i) -> p c i", i=NEAR)
                    .unsqueeze(2)
                    .to_broadcast([P, cut // NEAR, PACK, NEAR]),
                    op=ALU.mult,
                )

        def quantise(v):
            if tiles[v][0] == "down":
                b = tiles[v][1]
                if b == EARLY:
                    down_codes.append(
                        big.tile([P, LATE, BANK], U32, tag="big", align_bytes=64, name="late_codes")
                    )
                codes[v] = down_codes[b // EARLY][:, b % EARLY, :]
                plane[v] = down_plane[:, b, :]
                source = grouped[v][:, 0 : BANK * PACK]
            else:
                codes[v] = packed.tile([P, WORDS], U32, tag="codes", align_bytes=64, name="codes")[:]
                plane[v] = packed.tile([P, WORDS], U8, tag="plane", align_bytes=64, name="plane")[:]
                source = grouped[v][:]
            nc.vector.quantize_mx(out=codes[v].bitcast(FP8X4), scales=plane[v], in_=source)

        def multiply_gate_up(v):
            which, group, count, g0, passes = tiles[v]
            width = count * P
            for m in range(count):
                t = group + m
                if g0 == 0:
                    acc[which, t] = acc_pool.tile([P, TOKENS], F32, tag="acc", name="acc")
                for i in range(passes):
                    g = g0 + i
                    cols = slice(i * width + m * P, i * width + (m + 1) * P)
                    nc.tensor.matmul_mx(
                        out=acc[which, t][:],
                        lhsT=codes[v][:, cols].bitcast(FP8X4),
                        lhsT_scale=plane[v][:, cols],
                        rhs=x_codes[:, g, :].bitcast(FP8X4),
                        rhs_scale=x_plane[:, g, :],
                        start=(g == 0),
                        stop=(g == PASSES - 1),
                    )
            if g0 + passes < PASSES:
                return
            for m in range(count):
                t = group + m
                if which == 0:
                    nc.scalar.activation(
                        out=u_scaled[:, t, :],
                        in_=acc[which, t][:],
                        func=ACT.Copy,
                        scale=sizes[:, t : t + 1],
                    )
                else:
                    nc.scalar.activation(
                        out=swish[:, t, :],
                        in_=acc[which, t][:],
                        func=ACT.Silu,
                        scale=sizes[:, 4 + t : 5 + t],
                    )
            if v == last_gu:
                nc.vector.tensor_tensor(
                    out=h_grouped[:],
                    in0=swish[:].rearrange("p t b -> p b t"),
                    in1=u_scaled[:].rearrange("p t b -> p b t"),
                    op=ALU.mult,
                )
                nc.vector.quantize_mx(
                    out=h_codes[:].bitcast(FP8X4),
                    scales=h_plane[:],
                    in_=h_grouped[:].rearrange("p b t -> p (b t)"),
                )

        def multiply_down(b):
            o_bank = acc_pool.tile([P, BANK], F32, tag="acc", name="o_bank")
            nc.tensor.matmul_mx(
                out=o_bank[:],
                lhsT=h_codes[:].bitcast(FP8X4),
                lhsT_scale=h_plane[:],
                rhs=down_codes[b // EARLY][:, b % EARLY, :].bitcast(FP8X4),
                rhs_scale=down_plane[:, b, :],
                start=True,
                stop=True,
            )
            return o_bank

        def square_down(b):
            o_bank = multiply_down(b)
            squares = junk.tile([P, 2 * BANK], BF16, tag="squares")
            nc.scalar.activation(
                out=squares[:, 0:BANK], in_=o_bank[:], func=ACT.Square, accum_out=o_squares[:, b : b + 1]
            )

        for c in range(2):
            emit_steps(c + 1)
            prepare_x(c)
        emit_steps(ready["down", 0] + LAG)
        spreads[unit_of(tiles[0])] = spread_over_partitions(unit_of(tiles[0]))
        target = STEPS_AHEAD
        squared = 0
        for v in range(len(tiles) + 2):
            if v < len(tiles):
                scale(v)
            if 1 <= v <= len(tiles):
                quantise(v - 1)
            if v < 2:
                prepare_x(2 + v)
            if v == 2:
                prepare_gains()
            if v == D_PER_LOAD or v == 2 * D_PER_LOAD:
                load_gate_or_up(1)
            if v == 2 * D_PER_LOAD:
                load_down()
            if v == EARLY + 8:
                load_down()
            if v + 1 < len(tiles) and unit_of(tiles[v + 1]) not in spreads:
                unit = unit_of(tiles[v + 1])
                emit_steps(ready[unit] + LAG)
                spreads[unit] = spread_over_partitions(unit)
            target = target + (3 if v < EARLY else 4)
            emit_steps(target)
            if EARLY <= v - 2 <= last_gu:
                multiply_gate_up(v - 2)
            if v - 2 > last_gu:
                square_down(tiles[v - 2][1])
                for b in range(squared, min(squared + 2, EARLY)):
                    square_down(b)
                    squared = b + 1

        o_total = small.tile([P, 1], F32, tag="o_total")
        o_copied = small.tile([P, BLOCKS], F32, tag="o_copied")
        nc.scalar.activation(out=o_copied[:], in_=o_squares[:], func=ACT.Copy, accum_out=o_total[:])
        o_inverse = small.tile([P, 1], F32, tag="o_inverse")
        one_over_norm(o_inverse[:], o_total[:], 1)
        out_view = out.rearrange("b l d -> b (l d)")
        o_sb = [big.tile([P, D_MODEL // 2], F32, tag="big", align_bytes=64, name="o_sb") for n in range(2)]
        for b in range(BLOCKS):
            half = o_sb[b // (BLOCKS // 2)]
            first = (b % (BLOCKS // 2)) * BANK
            o_bank = multiply_down(b)
            if b % 2 == 0:
                nc.vector.tensor_scalar_mul(
                    out=half[:, first : first + BANK], in0=o_bank[:], scalar1=o_inverse[:, 0:1]
                )
            else:
                nc.scalar.activation(
                    out=half[:, first : first + BANK], in_=o_bank[:], func=ACT.Copy, scale=o_inverse[:, 0:1]
                )
                nc.sync.dma_start(
                    out=out_view[:, (b - 1) * BANK : (b + 1) * BANK],
                    in_=half[:, first - BANK : first + BANK],
                )
